import numpy as np
import ml_dtypes


def mxq(x, axis, fmt="e4m3"):
    dtype, down = {"e4m3": (ml_dtypes.float8_e4m3fn, 7), "e5m2": (ml_dtypes.float8_e5m2, 14)}[fmt]
    v = np.moveaxis(np.asarray(x, np.float32).astype(ml_dtypes.bfloat16).astype(np.float64), axis, -1)
    blocks = v.reshape(v.shape[:-1] + (-1, 32))
    amax = np.abs(blocks).max(-1, keepdims=True)
    byte = np.maximum(np.where(amax > 0, np.frexp(amax)[1] - 1 + 127, 0) - down, 1)
    scale = np.exp2(byte - 127.0)
    codes = (blocks / scale).astype(np.float32).astype(dtype).astype(np.float64)
    return np.moveaxis((codes * scale).reshape(v.shape), -1, axis)


WIDE = False


def mx_kscale(k):
    if not WIDE:
        return np.ones(k)
    levels = np.array([10, -10, 5, -5, 0])
    a = np.random.permutation(np.resize(levels, k // 512 * 4)).reshape(k // 512, 4)
    idx = np.arange(k)
    return np.exp2(a[idx // 512, idx % 128 // 32])


BF16 = ml_dtypes.bfloat16


def bf(x):
    return np.asarray(x, np.float32).astype(BF16)


def f64(x):
    return np.asarray(x).astype(np.float64)


B, D, C = 512, 128, 128
EPS_SQRT = 1e-10
EPS_NORM = 1e-12


def setup_inputs():
    s = mx_kscale(D * D)
    a = np.round(np.log2(np.array([s.max(), s.min()])) / 2)
    r = np.repeat(np.exp2(a - a.min()), D // 2)
    g = np.exp2(np.round(np.log2(np.mean(r ** 2))))
    return {"feat": bf(np.random.standard_normal((B, D)) * r ** 2),
            "W": bf(np.random.standard_normal((C, D * D)) * g / np.outer(r, r).reshape(-1)),
            "b": bf(np.random.standard_normal(C) * 0.3)}


def reference(feat, W, b):
    feat = f64(feat)
    x = (feat[:, :, None] * feat[:, None, :]).reshape(feat.shape[0], -1)
    x = np.sign(x) * np.sqrt(np.abs(x) + EPS_SQRT)
    norm = np.maximum(np.linalg.norm(x, axis=1, keepdims=True), EPS_NORM)
    x = x / norm
    return (mxq(x, 1, "e4m3") @ mxq(f64(W), 1, "e4m3").T) + f64(b)

@@ -1,0 +1,245 @@
+from contextlib import ExitStack
+
+import concourse.mybir as mybir
+from concourse.masks import make_identity
+
+F32 = mybir.dt.float32
+BF16 = mybir.dt.bfloat16
+U32 = mybir.dt.uint32
+U8 = mybir.dt.uint8
+FP8X4 = mybir.dt.float8_e4m3fn_x4
+ALU = mybir.AluOpType
+FUNC = mybir.ActivationFunctionType
+AXIS = mybir.AxisListType
+
+P = 128
+B, D, C = 512, 128, 128
+EPS_SQRT = 1e-10
+EPS_NORM = 1e-12
+
+BLOCKS = B // P
+K_PASS = 4 * P
+PASSES = D * D // K_PASS
+SLABS_PER_PASS = K_PASS // D
+PASSES_PER_ROUND = 4
+SLABS_PER_ROUND = PASSES_PER_ROUND * SLABS_PER_PASS
+ROUNDS_PER_BLOCK = PASSES // PASSES_PER_ROUND
+ROUNDS = BLOCKS * ROUNDS_PER_BLOCK
+ROUND_COLS = PASSES_PER_ROUND * K_PASS
+W_CHUNKS = PASSES // PASSES_PER_ROUND
+W_CHUNKS_ON_VECTOR = 3
+
+FLOPS = 2 * B * D * D * C
+
+
+def tile_bcnnresnet_k_kernel(tc, feat, W, b, out):
+    nc = tc.nc
+    with ExitStack() as ctx:
+        ctx.enter_context(tc.manual_schedule())
+        keep = ctx.enter_context(tc.tile_pool(name="keep", bufs=1))
+        w_in = ctx.enter_context(tc.tile_pool(name="w_in", bufs=W_CHUNKS))
+        roots_pool = ctx.enter_context(tc.tile_pool(name="roots_pool", bufs=6))
+        grouped_pool = ctx.enter_context(tc.tile_pool(name="grouped_pool", bufs=3))
+        codes_pool = ctx.enter_context(tc.tile_pool(name="codes_pool", bufs=3))
+        out_pool = ctx.enter_context(tc.tile_pool(name="out_pool", bufs=2))
+        banks_pool = ctx.enter_context(tc.psum_pool(name="banks_pool", bufs=6))
+        acc_pool = ctx.enter_context(tc.psum_pool(name="acc_pool", bufs=2))
+
+        feat_sb = keep.tile([P, BLOCKS, D], BF16, name="feat_sb")
+        nc.sync.dma_start(out=feat_sb[:], in_=feat.rearrange("(blk p) d -> p blk d", p=P))
+        w_rows = []
+        for q in range(W_CHUNKS):
+            rows = w_in.tile([P, ROUND_COLS], BF16, name="w_rows")
+            nc.sync.dma_start(out=rows[:], in_=W[:, q * ROUND_COLS : (q + 1) * ROUND_COLS])
+            w_rows.append(rows)
+        bias_rows = keep.tile([P, C], BF16, name="bias_rows")
+        nc.sync.dma_start(out=bias_rows[:], in_=b.partition_broadcast(P))
+
+        ident = keep.tile([P, P], F32, name="ident")
+        make_identity(nc, ident[:])
+
+        one = keep.tile([P, 1], F32, name="one")
+        nc.vector.memset(one[:], 1.0)
+        warm = keep.tile([P, 1], F32, name="warm")
+        nc.scalar.activation(out=warm[:], in_=one[:], func=FUNC.Sqrt)
+
+        mag = keep.tile([P, BLOCKS, D], BF16, name="mag")
+        sum_mag = keep.tile([P, BLOCKS], F32, name="sum_mag")
+        for blk in range(BLOCKS):
+            nc.scalar.activation(
+                out=mag[:, blk, :], in_=feat_sb[:, blk, :], func=FUNC.Abs, accum_out=sum_mag[:, blk : blk + 1]
+            )
+        nonzero = keep.tile([P, BLOCKS, D], BF16, name="nonzero")
+        nc.vector.tensor_single_scalar(out=nonzero[:], in_=feat_sb[:], scalar=0.0, op=ALU.not_equal)
+        count = keep.tile([P, BLOCKS], F32, name="count")
+        nc.vector.tensor_reduce(out=count[:], in_=nonzero[:], axis=AXIS.X, op=ALU.add)
+        count_sq = keep.tile([P, BLOCKS], F32, name="count_sq")
+        nc.vector.tensor_tensor(out=count_sq[:], in0=count[:], in1=count[:], op=ALU.mult)
+        norm_sq = keep.tile([P, BLOCKS], F32, name="norm_sq")
+        nc.vector.tensor_tensor(out=norm_sq[:], in0=sum_mag[:], in1=sum_mag[:], op=ALU.mult)
+        nc.vector.scalar_tensor_tensor(
+            out=norm_sq[:], in0=count_sq[:], scalar=EPS_SQRT, in1=norm_sq[:], op0=ALU.mult, op1=ALU.add
+        )
+        nc.vector.tensor_scalar_max(out=norm_sq[:], in0=norm_sq[:], scalar1=EPS_NORM * EPS_NORM)
+        inv_norm_sq = keep.tile([P, BLOCKS], F32, name="inv_norm_sq")
+        nc.vector.reciprocal(out=inv_norm_sq[:], in_=norm_sq[:])
+        eps_scaled = keep.tile([P, BLOCKS], F32, name="eps_scaled")
+        nc.vector.tensor_scalar_mul(out=eps_scaled[:], in0=inv_norm_sq[:], scalar1=EPS_SQRT)
+        slab_scale = keep.tile([P, BLOCKS, D], F32, name="slab_scale")
+
+        def scale_block(blk):
+            nc.vector.tensor_scalar_mul(
+                out=slab_scale[:, blk, :], in0=mag[:, blk, :], scalar1=inv_norm_sq[:, blk : blk + 1]
+            )
+
+        scale_block(0)
+
+        negative = keep.tile([P, BLOCKS, D], BF16, name="negative")
+        nc.vector.tensor_single_scalar(out=negative[:], in_=feat_sb[:], scalar=0.0, op=ALU.is_lt)
+        sign_f32 = keep.tile([P, BLOCKS, D], F32, name="sign_f32")
+        nc.vector.scalar_tensor_tensor(
+            out=sign_f32[:], in0=feat_sb[:], scalar=0.0, in1=negative[:], op0=ALU.is_gt, op1=ALU.subtract
+        )
+        sign_twice = keep.tile([P, BLOCKS, 2, D], BF16, name="sign_twice")
+        for half in range(2):
+            nc.vector.tensor_copy(out=sign_twice[:, :, half, :], in_=sign_f32[:])
+        for blk in range(1, BLOCKS):
+            scale_block(blk)
+
+        def transpose_words(words):
+            banks = []
+            for half in range(2):
+                bank = banks_pool.tile([P, 4, P], F32, name="bank")
+                for t in range(4):
+                    first = (4 * half + t) * P
+                    nc.tensor.transpose(out=bank[:, t, :], in_=words[:, first : first + P], identity=ident[:])
+                banks.append(bank)
+            return banks
+
+        row_sign = keep.tile([P, BLOCKS, P, 2], BF16, name="row_sign")
+        sign_bank = banks_pool.tile([P, 4, P], F32, name="bank")
+        for blk in range(BLOCKS):
+            nc.tensor.transpose(
+                out=sign_bank[:, blk, :],
+                in_=sign_twice[:, blk].rearrange("p h d -> p (h d)").bitcast(F32),
+                identity=ident[:],
+            )
+        nc.vector.tensor_copy(
+            out=row_sign[:].rearrange("p blk n e -> p (blk n e)").bitcast(F32),
+            in_=sign_bank[:].rearrange("p blk n -> p (blk n)"),
+        )
+
+        w_codes = keep.tile([P, PASSES, C], U32, name="w_codes", align_bytes=64)
+        w_scales = keep.tile([P, PASSES, C], U8, name="w_scales", align_bytes=64)
+
+        def pair_of_planes(banks, g):
+            return banks[g // 2][:, 2 * (g % 2) : 2 * (g % 2) + 2, :]
+
+        def take_roots(r):
+            blk, part = divmod(r, ROUNDS_PER_BLOCK)
+            roots = roots_pool.tile([P, SLABS_PER_ROUND, D], BF16, name="roots")
+            for s in range(SLABS_PER_ROUND):
+                i = part * SLABS_PER_ROUND + s
+                nc.scalar.activation(
+                    out=roots[:, s, :],
+                    in_=mag[:, blk, :],
+                    func=FUNC.Sqrt,
+                    scale=slab_scale[:, blk, i : i + 1],
+                    bias=eps_scaled[:, blk : blk + 1],
+                )
+            return roots
+
+        def sign_slabs(r, roots):
+            blk, part = divmod(r, ROUNDS_PER_BLOCK)
+            for s in range(SLABS_PER_ROUND):
+                i = part * SLABS_PER_ROUND + s
+                nc.vector.tensor_scalar_mul(
+                    out=roots[:, s, :], in0=roots[:, s, :], scalar1=sign_f32[:, blk, i : i + 1]
+                )
+
+        def regroup_x(r, banks):
+            blk = r // ROUNDS_PER_BLOCK
+            grouped = grouped_pool.tile([P, PASSES_PER_ROUND, P, 2, 2], BF16, name="grouped", align_bytes=64)
+            for g in range(PASSES_PER_ROUND):
+                nc.vector.tensor_tensor(
+                    out=grouped[:, g],
+                    in0=pair_of_planes(banks, g).bitcast(BF16).rearrange("p u (n e) -> p n u e", e=2),
+                    in1=row_sign[:, blk].unsqueeze(2).to_broadcast([P, P, 2, 2]),
+                    op=ALU.mult,
+                )
+            return grouped
+
+        def quantise_x(grouped):
+            codes = codes_pool.tile([P, PASSES_PER_ROUND * P], U32, name="x_codes", align_bytes=64)
+            scales = codes_pool.tile([P, PASSES_PER_ROUND * P], U8, name="x_scales", align_bytes=64)
+            nc.vector.quantize_mx(
+                out=codes[:].bitcast(FP8X4),
+                scales=scales[:],
+                in_=grouped[:].rearrange("p g n u e -> p (g n u e)"),
+            )
+            return codes, scales
+
+        def multiply(r, codes, scales, acc):
+            part = r % ROUNDS_PER_BLOCK
+            for g in range(PASSES_PER_ROUND):
+                k_pass = part * PASSES_PER_ROUND + g
+                cols = slice(g * P, (g + 1) * P)
+                nc.tensor.matmul_mx(
+                    out=acc[:],
+                    lhsT=codes[:, cols].bitcast(FP8X4),
+                    lhsT_scale=scales[:, cols],
+                    rhs=w_codes[:, k_pass, :].bitcast(FP8X4),
+                    rhs_scale=w_scales[:, k_pass, :],
+                    start=(k_pass == 0),
+                    stop=(k_pass == PASSES - 1),
+                )
+
+        def finish_block(blk, acc):
+            result = out_pool.tile([P, C], F32, name="result")
+            nc.vector.tensor_tensor(out=result[:], in0=acc[:], in1=bias_rows[:], op=ALU.add)
+            nc.sync.dma_start(out=out[blk * P : (blk + 1) * P, :], in_=result[:])
+
+        def regroup_w(q, banks):
+            grouped = grouped_pool.tile([P, PASSES_PER_ROUND, C, 2, 2], BF16, name="w_grouped", align_bytes=64)
+            for g in range(PASSES_PER_ROUND):
+                dst = grouped[:, g].rearrange("p c u e -> p c (u e)").bitcast(F32)
+                src = pair_of_planes(banks, g).rearrange("p u c -> p c u")
+                if q < W_CHUNKS_ON_VECTOR:
+                    nc.vector.tensor_copy(out=dst, in_=src)
+                else:
+                    nc.scalar.copy(out=dst, in_=src)
+            return grouped
+
+        def quantise_w(q, grouped):
+            passes = slice(q * PASSES_PER_ROUND, (q + 1) * PASSES_PER_ROUND)
+            nc.vector.quantize_mx(
+                out=w_codes[:, passes, :].rearrange("p g c -> p (g c)").bitcast(FP8X4),
+                scales=w_scales[:, passes, :].rearrange("p g c -> p (g c)"),
+                in_=grouped[:].rearrange("p g c u e -> p (g c u e)"),
+            )
+
+        roots_of, banks_of, grouped_of, w_grouped_of, acc_of = {}, {}, {}, {}, {}
+        for step in range(ROUNDS + 3):
+            if step < ROUNDS:
+                roots_of[step] = take_roots(step)
+            if step < W_CHUNKS:
+                w_banks = transpose_words(w_rows[step][:].bitcast(F32))
+                w_grouped_of[step] = regroup_w(step, w_banks)
+            r = step - 1
+            if 0 <= r < ROUNDS:
+                sign_slabs(r, roots_of[r])
+                banks_of[r] = transpose_words(roots_of[r][:].rearrange("p s d -> p (s d)").bitcast(F32))
+            r = step - 2
+            if 0 <= r < ROUNDS:
+                grouped_of[r] = regroup_x(r, banks_of[r])
+            if 0 <= step - 1 < W_CHUNKS:
+                quantise_w(step - 1, w_grouped_of[step - 1])
+            r = step - 3
+            if 0 <= r < ROUNDS:
+                blk, part = divmod(r, ROUNDS_PER_BLOCK)
+                codes, scales = quantise_x(grouped_of[r])
+                if part == 0:
+                    acc_of[blk] = acc_pool.tile([P, C], F32, name="acc")
+                multiply(r, codes, scales, acc_of[blk])
+                if part == ROUNDS_PER_BLOCK - 1:
+                    finish_block(blk, acc_of[blk])

@@ -21,13 +21,14 @@ BLOCKS = B // P
 K_PASS = 4 * P
 PASSES = D * D // K_PASS
 SLABS_PER_PASS = K_PASS // D
-PASSES_PER_ROUND = 4
-SLABS_PER_ROUND = PASSES_PER_ROUND * SLABS_PER_PASS
-ROUNDS_PER_BLOCK = PASSES // PASSES_PER_ROUND
-ROUNDS = BLOCKS * ROUNDS_PER_BLOCK
-ROUND_COLS = PASSES_PER_ROUND * K_PASS
-W_CHUNKS = PASSES // PASSES_PER_ROUND
-W_CHUNKS_ON_VECTOR = 3
+UNIT_PASSES = 2
+UNIT_SLABS = UNIT_PASSES * SLABS_PER_PASS
+UNIT_COLS = UNIT_PASSES * K_PASS
+UNITS_PER_BLOCK = PASSES // UNIT_PASSES
+UNITS = BLOCKS * UNITS_PER_BLOCK
+W_UNITS = PASSES // UNIT_PASSES
+W_LOADS = 8
+W_UNITS_AHEAD = 3
 
 FLOPS = 2 * B * D * D * C
 
@@ -37,20 +38,21 @@ def tile_bcnnresnet_k_kernel(tc, feat, W, b, out):
     with ExitStack() as ctx:
         ctx.enter_context(tc.manual_schedule())
         keep = ctx.enter_context(tc.tile_pool(name="keep", bufs=1))
-        w_in = ctx.enter_context(tc.tile_pool(name="w_in", bufs=W_CHUNKS))
-        roots_pool = ctx.enter_context(tc.tile_pool(name="roots_pool", bufs=6))
-        grouped_pool = ctx.enter_context(tc.tile_pool(name="grouped_pool", bufs=3))
-        codes_pool = ctx.enter_context(tc.tile_pool(name="codes_pool", bufs=3))
+        w_in = ctx.enter_context(tc.tile_pool(name="w_in", bufs=W_LOADS))
+        roots_pool = ctx.enter_context(tc.tile_pool(name="roots_pool", bufs=8))
+        grouped_pool = ctx.enter_context(tc.tile_pool(name="grouped_pool", bufs=4))
+        codes_pool = ctx.enter_context(tc.tile_pool(name="codes_pool", bufs=6))
         out_pool = ctx.enter_context(tc.tile_pool(name="out_pool", bufs=2))
         banks_pool = ctx.enter_context(tc.psum_pool(name="banks_pool", bufs=6))
         acc_pool = ctx.enter_context(tc.psum_pool(name="acc_pool", bufs=2))
 
         feat_sb = keep.tile([P, BLOCKS, D], BF16, name="feat_sb")
         nc.sync.dma_start(out=feat_sb[:], in_=feat.rearrange("(blk p) d -> p blk d", p=P))
+        load_cols = D * D // W_LOADS
         w_rows = []
-        for q in range(W_CHUNKS):
-            rows = w_in.tile([P, ROUND_COLS], BF16, name="w_rows")
-            nc.sync.dma_start(out=rows[:], in_=W[:, q * ROUND_COLS : (q + 1) * ROUND_COLS])
+        for q in range(W_LOADS):
+            rows = w_in.tile([P, load_cols], BF16, name="w_rows")
+            nc.sync.dma_start(out=rows[:], in_=W[:, q * load_cols : (q + 1) * load_cols])
             w_rows.append(rows)
         bias_rows = keep.tile([P, C], BF16, name="bias_rows")
         nc.sync.dma_start(out=bias_rows[:], in_=b.partition_broadcast(P))
@@ -63,28 +65,67 @@ def tile_bcnnresnet_k_kernel(tc, feat, W, b, out):
         warm = keep.tile([P, 1], F32, name="warm")
         nc.scalar.activation(out=warm[:], in_=one[:], func=FUNC.Sqrt)
 
+        w_codes = keep.tile([P, PASSES, C], U32, name="w_codes", align_bytes=64)
+        w_scales = keep.tile([P, PASSES, C], U8, name="w_scales", align_bytes=64)
+
+        def transpose_unit(words):
+            bank = banks_pool.tile([P, 2, UNIT_PASSES, P], F32, name="bank")
+            for g in range(UNIT_PASSES):
+                for u in range(2):
+                    first = (2 * g + u) * P
+                    nc.tensor.transpose(out=bank[:, u, g, :], in_=words[:, first : first + P], identity=ident[:])
+            return bank
+
+        def transpose_w(w):
+            per_load = W_UNITS // W_LOADS
+            rows = w_rows[w // per_load]
+            first = (w % per_load) * UNIT_COLS
+            return transpose_unit(rows[:, first : first + UNIT_COLS].bitcast(F32))
+
+        def regroup_w(bank):
+            grouped = grouped_pool.tile([P, UNIT_PASSES, C, 2, 2], BF16, name="w_grouped", align_bytes=64)
+            nc.scalar.copy(
+                out=grouped[:].rearrange("p g c u e -> p (g c) (u e)").bitcast(F32),
+                in_=bank[:].rearrange("p u g c -> p (g c) u"),
+            )
+            return grouped
+
+        def quantise_w(w, grouped):
+            passes = slice(w * UNIT_PASSES, (w + 1) * UNIT_PASSES)
+            nc.vector.quantize_mx(
+                out=w_codes[:, passes, :].rearrange("p g c -> p (g c)").bitcast(FP8X4),
+                scales=w_scales[:, passes, :].rearrange("p g c -> p (g c)"),
+                in_=grouped[:].rearrange("p g c u e -> p (g c u e)"),
+            )
+
         mag = keep.tile([P, BLOCKS, D], BF16, name="mag")
         sum_mag = keep.tile([P, BLOCKS], F32, name="sum_mag")
         for blk in range(BLOCKS):
             nc.scalar.activation(
                 out=mag[:, blk, :], in_=feat_sb[:, blk, :], func=FUNC.Abs, accum_out=sum_mag[:, blk : blk + 1]
             )
+        w_bank_of, w_grouped_of = {}, {}
+        for w in range(W_UNITS_AHEAD):
+            w_bank_of[w] = transpose_w(w)
+            w_grouped_of[w] = regroup_w(w_bank_of[w])
+        w_bank_of[W_UNITS_AHEAD] = transpose_w(W_UNITS_AHEAD)
+
         nonzero = keep.tile([P, BLOCKS, D], BF16, name="nonzero")
         nc.vector.tensor_single_scalar(out=nonzero[:], in_=feat_sb[:], scalar=0.0, op=ALU.not_equal)
         count = keep.tile([P, BLOCKS], F32, name="count")
         nc.vector.tensor_reduce(out=count[:], in_=nonzero[:], axis=AXIS.X, op=ALU.add)
         count_sq = keep.tile([P, BLOCKS], F32, name="count_sq")
         nc.vector.tensor_tensor(out=count_sq[:], in0=count[:], in1=count[:], op=ALU.mult)
+        sum_sq = keep.tile([P, BLOCKS], F32, name="sum_sq")
+        nc.vector.tensor_tensor(out=sum_sq[:], in0=sum_mag[:], in1=sum_mag[:], op=ALU.mult)
         norm_sq = keep.tile([P, BLOCKS], F32, name="norm_sq")
-        nc.vector.tensor_tensor(out=norm_sq[:], in0=sum_mag[:], in1=sum_mag[:], op=ALU.mult)
         nc.vector.scalar_tensor_tensor(
-            out=norm_sq[:], in0=count_sq[:], scalar=EPS_SQRT, in1=norm_sq[:], op0=ALU.mult, op1=ALU.add
+            out=norm_sq[:], in0=count_sq[:], scalar=EPS_SQRT, in1=sum_sq[:], op0=ALU.mult, op1=ALU.add
         )
-        nc.vector.tensor_scalar_max(out=norm_sq[:], in0=norm_sq[:], scalar1=EPS_NORM * EPS_NORM)
+        clamped = keep.tile([P, BLOCKS], F32, name="clamped")
+        nc.vector.tensor_scalar_max(out=clamped[:], in0=norm_sq[:], scalar1=EPS_NORM * EPS_NORM)
         inv_norm_sq = keep.tile([P, BLOCKS], F32, name="inv_norm_sq")
-        nc.vector.reciprocal(out=inv_norm_sq[:], in_=norm_sq[:])
-        eps_scaled = keep.tile([P, BLOCKS], F32, name="eps_scaled")
-        nc.vector.tensor_scalar_mul(out=eps_scaled[:], in0=inv_norm_sq[:], scalar1=EPS_SQRT)
+        nc.vector.reciprocal(out=inv_norm_sq[:], in_=clamped[:])
         slab_scale = keep.tile([P, BLOCKS, D], F32, name="slab_scale")
 
         def scale_block(blk):
@@ -93,6 +134,8 @@ def tile_bcnnresnet_k_kernel(tc, feat, W, b, out):
             )
 
         scale_block(0)
+        eps_scaled = keep.tile([P, BLOCKS], F32, name="eps_scaled")
+        nc.vector.tensor_scalar_mul(out=eps_scaled[:], in0=inv_norm_sq[:], scalar1=EPS_SQRT)
 
         negative = keep.tile([P, BLOCKS, D], BF16, name="negative")
         nc.vector.tensor_single_scalar(out=negative[:], in_=feat_sb[:], scalar=0.0, op=ALU.is_lt)
@@ -101,45 +144,30 @@ def tile_bcnnresnet_k_kernel(tc, feat, W, b, out):
             out=sign_f32[:], in0=feat_sb[:], scalar=0.0, in1=negative[:], op0=ALU.is_gt, op1=ALU.subtract
         )
         sign_twice = keep.tile([P, BLOCKS, 2, D], BF16, name="sign_twice")
-        for half in range(2):
-            nc.vector.tensor_copy(out=sign_twice[:, :, half, :], in_=sign_f32[:])
-        for blk in range(1, BLOCKS):
-            scale_block(blk)
+        nc.vector.tensor_copy(out=sign_twice[:], in_=sign_f32[:].unsqueeze(2).to_broadcast([P, BLOCKS, 2, D]))
 
-        def transpose_words(words):
-            banks = []
-            for half in range(2):
-                bank = banks_pool.tile([P, 4, P], F32, name="bank")
-                for t in range(4):
-                    first = (4 * half + t) * P
-                    nc.tensor.transpose(out=bank[:, t, :], in_=words[:, first : first + P], identity=ident[:])
-                banks.append(bank)
-            return banks
-
-        row_sign = keep.tile([P, BLOCKS, P, 2], BF16, name="row_sign")
-        sign_bank = banks_pool.tile([P, 4, P], F32, name="bank")
+        sign_bank = banks_pool.tile([P, BLOCKS, P], F32, name="bank")
         for blk in range(BLOCKS):
             nc.tensor.transpose(
                 out=sign_bank[:, blk, :],
                 in_=sign_twice[:, blk].rearrange("p h d -> p (h d)").bitcast(F32),
                 identity=ident[:],
             )
+        row_sign = keep.tile([P, BLOCKS, UNIT_PASSES, P, 2], BF16, name="row_sign")
         nc.vector.tensor_copy(
-            out=row_sign[:].rearrange("p blk n e -> p (blk n e)").bitcast(F32),
-            in_=sign_bank[:].rearrange("p blk n -> p (blk n)"),
+            out=row_sign[:].rearrange("p blk g n e -> p blk g (n e)").bitcast(F32),
+            in_=sign_bank[:].unsqueeze(2).to_broadcast([P, BLOCKS, UNIT_PASSES, P]),
         )
+        for blk in range(1, BLOCKS):
+            scale_block(blk)
+        for w in range(W_UNITS_AHEAD):
+            quantise_w(w, w_grouped_of[w])
 
-        w_codes = keep.tile([P, PASSES, C], U32, name="w_codes", align_bytes=64)
-        w_scales = keep.tile([P, PASSES, C], U8, name="w_scales", align_bytes=64)
-
-        def pair_of_planes(banks, g):
-            return banks[g // 2][:, 2 * (g % 2) : 2 * (g % 2) + 2, :]
-
-        def take_roots(r):
-            blk, part = divmod(r, ROUNDS_PER_BLOCK)
-            roots = roots_pool.tile([P, SLABS_PER_ROUND, D], BF16, name="roots")
-            for s in range(SLABS_PER_ROUND):
-                i = part * SLABS_PER_ROUND + s
+        def take_roots(h):
+            blk, part = divmod(h, UNITS_PER_BLOCK)
+            roots = roots_pool.tile([P, UNIT_SLABS, D], BF16, name="roots")
+            for s in range(UNIT_SLABS):
+                i = part * UNIT_SLABS + s
                 nc.scalar.activation(
                     out=roots[:, s, :],
                     in_=mag[:, blk, :],
@@ -149,45 +177,46 @@ def tile_bcnnresnet_k_kernel(tc, feat, W, b, out):
                 )
             return roots
 
-        def sign_slabs(r, roots):
-            blk, part = divmod(r, ROUNDS_PER_BLOCK)
-            for s in range(SLABS_PER_ROUND):
-                i = part * SLABS_PER_ROUND + s
+        def sign_slabs(h, roots):
+            blk, part = divmod(h, UNITS_PER_BLOCK)
+            for s in range(UNIT_SLABS):
+                i = part * UNIT_SLABS + s
                 nc.vector.tensor_scalar_mul(
                     out=roots[:, s, :], in0=roots[:, s, :], scalar1=sign_f32[:, blk, i : i + 1]
                 )
 
-        def regroup_x(r, banks):
-            blk = r // ROUNDS_PER_BLOCK
-            grouped = grouped_pool.tile([P, PASSES_PER_ROUND, P, 2, 2], BF16, name="grouped", align_bytes=64)
-            for g in range(PASSES_PER_ROUND):
-                nc.vector.tensor_tensor(
-                    out=grouped[:, g],
-                    in0=pair_of_planes(banks, g).bitcast(BF16).rearrange("p u (n e) -> p n u e", e=2),
-                    in1=row_sign[:, blk].unsqueeze(2).to_broadcast([P, P, 2, 2]),
-                    op=ALU.mult,
-                )
+        def regroup_x(h, bank):
+            blk = h // UNITS_PER_BLOCK
+            grouped = grouped_pool.tile([P, UNIT_PASSES, P, 2, 2], BF16, name="grouped", align_bytes=64)
+            nc.vector.tensor_tensor(
+                out=grouped[:].rearrange("p g n u e -> p (g n) u e"),
+                in0=bank[:].bitcast(BF16).rearrange("p u g (n e) -> p (g n) u e", e=2),
+                in1=row_sign[:, blk]
+                .rearrange("p g n e -> p (g n) e")
+                .unsqueeze(2)
+                .to_broadcast([P, UNIT_PASSES * P, 2, 2]),
+                op=ALU.mult,
+            )
             return grouped
 
         def quantise_x(grouped):
-            codes = codes_pool.tile([P, PASSES_PER_ROUND * P], U32, name="x_codes", align_bytes=64)
-            scales = codes_pool.tile([P, PASSES_PER_ROUND * P], U8, name="x_scales", align_bytes=64)
+            codes = codes_pool.tile([P, UNIT_PASSES, P], U32, name="x_codes", align_bytes=64)
+            scales = codes_pool.tile([P, UNIT_PASSES, P], U8, name="x_scales", align_bytes=64)
             nc.vector.quantize_mx(
-                out=codes[:].bitcast(FP8X4),
-                scales=scales[:],
+                out=codes[:].rearrange("p g n -> p (g n)").bitcast(FP8X4),
+                scales=scales[:].rearrange("p g n -> p (g n)"),
                 in_=grouped[:].rearrange("p g n u e -> p (g n u e)"),
             )
             return codes, scales
 
-        def multiply(r, codes, scales, acc):
-            part = r % ROUNDS_PER_BLOCK
-            for g in range(PASSES_PER_ROUND):
-                k_pass = part * PASSES_PER_ROUND + g
-                cols = slice(g * P, (g + 1) * P)
+        def multiply(h, codes, scales, acc):
+            part = h % UNITS_PER_BLOCK
+            for g in range(UNIT_PASSES):
+                k_pass = part * UNIT_PASSES + g
                 nc.tensor.matmul_mx(
                     out=acc[:],
-                    lhsT=codes[:, cols].bitcast(FP8X4),
-                    lhsT_scale=scales[:, cols],
+                    lhsT=codes[:, g, :].bitcast(FP8X4),
+                    lhsT_scale=scales[:, g, :],
                     rhs=w_codes[:, k_pass, :].bitcast(FP8X4),
                     rhs_scale=w_scales[:, k_pass, :],
                     start=(k_pass == 0),
@@ -199,47 +228,33 @@ def tile_bcnnresnet_k_kernel(tc, feat, W, b, out):
             nc.vector.tensor_tensor(out=result[:], in0=acc[:], in1=bias_rows[:], op=ALU.add)
             nc.sync.dma_start(out=out[blk * P : (blk + 1) * P, :], in_=result[:])
 
-        def regroup_w(q, banks):
-            grouped = grouped_pool.tile([P, PASSES_PER_ROUND, C, 2, 2], BF16, name="w_grouped", align_bytes=64)
-            for g in range(PASSES_PER_ROUND):
-                dst = grouped[:, g].rearrange("p c u e -> p c (u e)").bitcast(F32)
-                src = pair_of_planes(banks, g).rearrange("p u c -> p c u")
-                if q < W_CHUNKS_ON_VECTOR:
-                    nc.vector.tensor_copy(out=dst, in_=src)
-                else:
-                    nc.scalar.copy(out=dst, in_=src)
-            return grouped
-
-        def quantise_w(q, grouped):
-            passes = slice(q * PASSES_PER_ROUND, (q + 1) * PASSES_PER_ROUND)
-            nc.vector.quantize_mx(
-                out=w_codes[:, passes, :].rearrange("p g c -> p (g c)").bitcast(FP8X4),
-                scales=w_scales[:, passes, :].rearrange("p g c -> p (g c)"),
-                in_=grouped[:].rearrange("p g c u e -> p (g c u e)"),
-            )
-
-        roots_of, banks_of, grouped_of, w_grouped_of, acc_of = {}, {}, {}, {}, {}
-        for step in range(ROUNDS + 3):
-            if step < ROUNDS:
+        roots_of, bank_of, grouped_of, codes_of, acc_of = {}, {}, {}, {}, {}
+        for step in range(UNITS + 5):
+            w = step + W_UNITS_AHEAD
+            if w < W_UNITS:
+                w_grouped_of[w] = regroup_w(w_bank_of[w])
+            if step < UNITS:
                 roots_of[step] = take_roots(step)
-            if step < W_CHUNKS:
-                w_banks = transpose_words(w_rows[step][:].bitcast(F32))
-                w_grouped_of[step] = regroup_w(step, w_banks)
-            r = step - 1
-            if 0 <= r < ROUNDS:
-                sign_slabs(r, roots_of[r])
-                banks_of[r] = transpose_words(roots_of[r][:].rearrange("p s d -> p (s d)").bitcast(F32))
-            r = step - 2
-            if 0 <= r < ROUNDS:
-                grouped_of[r] = regroup_x(r, banks_of[r])
-            if 0 <= step - 1 < W_CHUNKS:
-                quantise_w(step - 1, w_grouped_of[step - 1])
-            r = step - 3
-            if 0 <= r < ROUNDS:
-                blk, part = divmod(r, ROUNDS_PER_BLOCK)
-                codes, scales = quantise_x(grouped_of[r])
-                if part == 0:
+            h = step - 1
+            if 0 <= h < UNITS:
+                sign_slabs(h, roots_of[h])
+                bank_of[h] = transpose_unit(roots_of[h][:].rearrange("p s d -> p (s d)").bitcast(F32))
+            if w + 1 < W_UNITS:
+                w_bank_of[w + 1] = transpose_w(w + 1)
+            h = step - 5
+            if 0 <= h < UNITS and h % UNITS_PER_BLOCK == UNITS_PER_BLOCK - 1:
+                finish_block(h // UNITS_PER_BLOCK, acc_of[h // UNITS_PER_BLOCK])
+            h = step - 2
+            if 0 <= h < UNITS:
+                grouped_of[h] = regroup_x(h, bank_of[h])
+            h = step - 3
+            if 0 <= h < UNITS:
+                codes_of[h] = quantise_x(grouped_of[h])
+            if w < W_UNITS:
+                quantise_w(w, w_grouped_of[w])
+            if 0 <= h < UNITS and h % 2 == 1:
+                blk = h // UNITS_PER_BLOCK
+                if h % UNITS_PER_BLOCK == 1:
                     acc_of[blk] = acc_pool.tile([P, C], F32, name="acc")
-                multiply(r, codes, scales, acc_of[blk])
-                if part == ROUNDS_PER_BLOCK - 1:
-                    finish_block(blk, acc_of[blk])
+                for unit in (h - 1, h):
+                    multiply(unit, codes_of[unit][0], codes_of[unit][1], acc_of[blk])

@@ -14,21 +14,21 @@ AXIS = mybir.AxisListType
 
 P = 128
 B, D, C = 512, 128, 128
+H = D // 2
 EPS_SQRT = 1e-10
 EPS_NORM = 1e-12
 
 BLOCKS = B // P
 K_PASS = 4 * P
 PASSES = D * D // K_PASS
-SLABS_PER_PASS = K_PASS // D
 UNIT_PASSES = 2
-UNIT_SLABS = UNIT_PASSES * SLABS_PER_PASS
-UNIT_COLS = UNIT_PASSES * K_PASS
+UNIT_ROWS = 8
 UNITS_PER_BLOCK = PASSES // UNIT_PASSES
-UNITS = BLOCKS * UNITS_PER_BLOCK
-W_UNITS = PASSES // UNIT_PASSES
+HALF_UNITS = UNITS_PER_BLOCK // 2
+STEPS = BLOCKS * UNITS_PER_BLOCK
+W_UNITS = UNITS_PER_BLOCK
 W_LOADS = 8
-W_UNITS_AHEAD = 3
+W_AHEAD = 3
 
 FLOPS = 2 * B * D * D * C
 
@@ -39,12 +39,13 @@ def tile_bcnnresnet_k_kernel(tc, feat, W, b, out):
         ctx.enter_context(tc.manual_schedule())
         keep = ctx.enter_context(tc.tile_pool(name="keep", bufs=1))
         w_in = ctx.enter_context(tc.tile_pool(name="w_in", bufs=W_LOADS))
-        roots_pool = ctx.enter_context(tc.tile_pool(name="roots_pool", bufs=8))
+        table_pool = ctx.enter_context(tc.tile_pool(name="table_pool", bufs=2))
+        col_sign_pool = ctx.enter_context(tc.tile_pool(name="col_sign_pool", bufs=2))
         grouped_pool = ctx.enter_context(tc.tile_pool(name="grouped_pool", bufs=4))
-        codes_pool = ctx.enter_context(tc.tile_pool(name="codes_pool", bufs=6))
+        codes_pool = ctx.enter_context(tc.tile_pool(name="codes_pool", bufs=20))
         out_pool = ctx.enter_context(tc.tile_pool(name="out_pool", bufs=2))
-        banks_pool = ctx.enter_context(tc.psum_pool(name="banks_pool", bufs=6))
-        acc_pool = ctx.enter_context(tc.psum_pool(name="acc_pool", bufs=2))
+        banks_pool = ctx.enter_context(tc.psum_pool(name="banks_pool", bufs=5))
+        acc_pool = ctx.enter_context(tc.psum_pool(name="acc_pool", bufs=3))
 
         feat_sb = keep.tile([P, BLOCKS, D], BF16, name="feat_sb")
         nc.sync.dma_start(out=feat_sb[:], in_=feat.rearrange("(blk p) d -> p blk d", p=P))
@@ -59,6 +60,8 @@ def tile_bcnnresnet_k_kernel(tc, feat, W, b, out):
 
         ident = keep.tile([P, P], F32, name="ident")
         make_identity(nc, ident[:])
+        ident_bf = keep.tile([P, P], BF16, name="ident_bf")
+        make_identity(nc, ident_bf[:])
 
         one = keep.tile([P, 1], F32, name="one")
         nc.vector.memset(one[:], 1.0)
@@ -68,7 +71,7 @@ def tile_bcnnresnet_k_kernel(tc, feat, W, b, out):
         w_codes = keep.tile([P, PASSES, C], U32, name="w_codes", align_bytes=64)
         w_scales = keep.tile([P, PASSES, C], U8, name="w_scales", align_bytes=64)
 
-        def transpose_unit(words):
+        def transpose_rows(words):
             bank = banks_pool.tile([P, 2, UNIT_PASSES, P], F32, name="bank")
             for g in range(UNIT_PASSES):
                 for u in range(2):
@@ -76,18 +79,38 @@ def tile_bcnnresnet_k_kernel(tc, feat, W, b, out):
                     nc.tensor.transpose(out=bank[:, u, g, :], in_=words[:, first : first + P], identity=ident[:])
             return bank
 
+        def transpose_cols(table, i0):
+            words = table[:].rearrange("p m c -> p (m c)").bitcast(F32).rearrange("p (m w) -> p m w", m=D)
+            bank = banks_pool.tile([P, 2, UNIT_PASSES, P], F32, name="bank")
+            for g in range(UNIT_PASSES):
+                for u in range(2):
+                    nc.tensor.transpose(out=bank[:, u, g, :], in_=words[:, :, i0 // 2 + 2 * g + u], identity=ident[:])
+            return bank
+
         def transpose_w(w):
             per_load = W_UNITS // W_LOADS
             rows = w_rows[w // per_load]
-            first = (w % per_load) * UNIT_COLS
-            return transpose_unit(rows[:, first : first + UNIT_COLS].bitcast(F32))
+            first = (w % per_load) * UNIT_ROWS * D
+            if w < HALF_UNITS:
+                return transpose_rows(rows[:, first : first + UNIT_ROWS * D].bitcast(F32))
+            bank = banks_pool.tile([P, UNIT_PASSES, 4, P], BF16, name="bank")
+            for g in range(UNIT_PASSES):
+                for t in range(4):
+                    at = first + (4 * g + t) * D
+                    nc.tensor.transpose(out=bank[:, g, t, :], in_=rows[:, at : at + D], identity=ident_bf[:])
+            return bank
 
-        def regroup_w(bank):
-            grouped = grouped_pool.tile([P, UNIT_PASSES, C, 2, 2], BF16, name="w_grouped", align_bytes=64)
-            nc.scalar.copy(
-                out=grouped[:].rearrange("p g c u e -> p (g c) (u e)").bitcast(F32),
-                in_=bank[:].rearrange("p u g c -> p (g c) u"),
-            )
+        def regroup_w(w, bank):
+            grouped = grouped_pool.tile([P, UNIT_PASSES, C, 4], BF16, name="w_grouped", align_bytes=64)
+            if w < HALF_UNITS:
+                words_out = grouped[:].rearrange("p g c t -> p (g c) t").bitcast(F32)
+                words_in = bank[:].rearrange("p u g c -> p (g c) u")
+                if w < W_AHEAD:
+                    nc.scalar.copy(out=words_out, in_=words_in)
+                else:
+                    nc.vector.tensor_copy(out=words_out, in_=words_in)
+            else:
+                nc.scalar.copy(out=grouped[:], in_=bank[:].rearrange("p g t c -> p g c t"))
             return grouped
 
         def quantise_w(w, grouped):
@@ -95,7 +118,7 @@ def tile_bcnnresnet_k_kernel(tc, feat, W, b, out):
             nc.vector.quantize_mx(
                 out=w_codes[:, passes, :].rearrange("p g c -> p (g c)").bitcast(FP8X4),
                 scales=w_scales[:, passes, :].rearrange("p g c -> p (g c)"),
-                in_=grouped[:].rearrange("p g c u e -> p (g c u e)"),
+                in_=grouped[:].rearrange("p g c t -> p (g c t)"),
             )
 
         mag = keep.tile([P, BLOCKS, D], BF16, name="mag")
@@ -105,10 +128,10 @@ def tile_bcnnresnet_k_kernel(tc, feat, W, b, out):
                 out=mag[:, blk, :], in_=feat_sb[:, blk, :], func=FUNC.Abs, accum_out=sum_mag[:, blk : blk + 1]
             )
         w_bank_of, w_grouped_of = {}, {}
-        for w in range(W_UNITS_AHEAD):
+        for w in range(W_AHEAD):
             w_bank_of[w] = transpose_w(w)
-            w_grouped_of[w] = regroup_w(w_bank_of[w])
-        w_bank_of[W_UNITS_AHEAD] = transpose_w(W_UNITS_AHEAD)
+            w_grouped_of[w] = regroup_w(w, w_bank_of[w])
+        w_bank_of[W_AHEAD] = transpose_w(W_AHEAD)
 
         nonzero = keep.tile([P, BLOCKS, D], BF16, name="nonzero")
         nc.vector.tensor_single_scalar(out=nonzero[:], in_=feat_sb[:], scalar=0.0, op=ALU.not_equal)
@@ -126,11 +149,11 @@ def tile_bcnnresnet_k_kernel(tc, feat, W, b, out):
         nc.vector.tensor_scalar_max(out=clamped[:], in0=norm_sq[:], scalar1=EPS_NORM * EPS_NORM)
         inv_norm_sq = keep.tile([P, BLOCKS], F32, name="inv_norm_sq")
         nc.vector.reciprocal(out=inv_norm_sq[:], in_=clamped[:])
-        slab_scale = keep.tile([P, BLOCKS, D], F32, name="slab_scale")
+        row_scale = keep.tile([P, BLOCKS, D], F32, name="row_scale")
 
         def scale_block(blk):
             nc.vector.tensor_scalar_mul(
-                out=slab_scale[:, blk, :], in0=mag[:, blk, :], scalar1=inv_norm_sq[:, blk : blk + 1]
+                out=row_scale[:, blk, :], in0=mag[:, blk, :], scalar1=inv_norm_sq[:, blk : blk + 1]
             )
 
         scale_block(0)
@@ -146,6 +169,23 @@ def tile_bcnnresnet_k_kernel(tc, feat, W, b, out):
         sign_twice = keep.tile([P, BLOCKS, 2, D], BF16, name="sign_twice")
         nc.vector.tensor_copy(out=sign_twice[:], in_=sign_f32[:].unsqueeze(2).to_broadcast([P, BLOCKS, 2, D]))
 
+        sign_high = keep.tile([P, BLOCKS, H], BF16, name="sign_high")
+        nc.vector.tensor_copy(out=sign_high[:], in_=sign_f32[:, :, H:])
+        words_high = P * H // 2
+        parked = out[(BLOCKS - 1) * P :, :].rearrange("r c -> (r c)")
+        nc.sync.dma_start(
+            out=parked.rearrange("(blk n w) -> n blk w", blk=BLOCKS, n=P), in_=sign_high[:].bitcast(F32)
+        )
+        col_sign_of = {}
+
+        def load_col_sign(blk):
+            col_sign = col_sign_pool.tile([P, P, H], BF16, name="col_sign")
+            nc.sync.dma_start(
+                out=col_sign[:].rearrange("p n i -> p (n i)").bitcast(F32),
+                in_=parked[blk * words_high : (blk + 1) * words_high].partition_broadcast(P),
+            )
+            col_sign_of[blk] = col_sign
+
         sign_bank = banks_pool.tile([P, BLOCKS, P], F32, name="bank")
         for blk in range(BLOCKS):
             nc.tensor.transpose(
@@ -160,43 +200,66 @@ def tile_bcnnresnet_k_kernel(tc, feat, W, b, out):
         )
         for blk in range(1, BLOCKS):
             scale_block(blk)
-        for w in range(W_UNITS_AHEAD):
+        for w in range(W_AHEAD):
             quantise_w(w, w_grouped_of[w])
 
-        def take_roots(h):
-            blk, part = divmod(h, UNITS_PER_BLOCK)
-            roots = roots_pool.tile([P, UNIT_SLABS, D], BF16, name="roots")
-            for s in range(UNIT_SLABS):
-                i = part * UNIT_SLABS + s
+        table_of = {}
+
+        def columns_from(i):
+            return 0 if i < H else H
+
+        def take_roots(step):
+            blk, part = divmod(step, UNITS_PER_BLOCK)
+            if part == 0:
+                table_of[blk] = table_pool.tile([P, D, D], BF16, name="table")
+            for i in range(part * UNIT_ROWS, (part + 1) * UNIT_ROWS):
+                j0 = columns_from(i)
                 nc.scalar.activation(
-                    out=roots[:, s, :],
-                    in_=mag[:, blk, :],
+                    out=table_of[blk][:, i, j0:],
+                    in_=mag[:, blk, j0:],
                     func=FUNC.Sqrt,
-                    scale=slab_scale[:, blk, i : i + 1],
+                    scale=row_scale[:, blk, i : i + 1],
                     bias=eps_scaled[:, blk : blk + 1],
                 )
-            return roots
 
-        def sign_slabs(h, roots):
+        def sign_rows(step):
+            blk, part = divmod(step, UNITS_PER_BLOCK)
+            for i in range(part * UNIT_ROWS, (part + 1) * UNIT_ROWS):
+                row = table_of[blk][:, i, columns_from(i) :]
+                nc.vector.tensor_scalar_mul(out=row, in0=row, scalar1=sign_f32[:, blk, i : i + 1])
+
+        def transpose_x(h):
             blk, part = divmod(h, UNITS_PER_BLOCK)
-            for s in range(UNIT_SLABS):
-                i = part * UNIT_SLABS + s
-                nc.vector.tensor_scalar_mul(
-                    out=roots[:, s, :], in0=roots[:, s, :], scalar1=sign_f32[:, blk, i : i + 1]
+            i0 = part * UNIT_ROWS
+            if part < HALF_UNITS:
+                return transpose_rows(
+                    table_of[blk][:, i0 : i0 + UNIT_ROWS, :].rearrange("p s d -> p (s d)").bitcast(F32)
                 )
+            return transpose_cols(table_of[blk], i0)
 
         def regroup_x(h, bank):
-            blk = h // UNITS_PER_BLOCK
+            blk, part = divmod(h, UNITS_PER_BLOCK)
             grouped = grouped_pool.tile([P, UNIT_PASSES, P, 2, 2], BF16, name="grouped", align_bytes=64)
-            nc.vector.tensor_tensor(
-                out=grouped[:].rearrange("p g n u e -> p (g n) u e"),
-                in0=bank[:].bitcast(BF16).rearrange("p u g (n e) -> p (g n) u e", e=2),
-                in1=row_sign[:, blk]
-                .rearrange("p g n e -> p (g n) e")
-                .unsqueeze(2)
-                .to_broadcast([P, UNIT_PASSES * P, 2, 2]),
-                op=ALU.mult,
-            )
+            if part < HALF_UNITS:
+                nc.vector.tensor_tensor(
+                    out=grouped[:].rearrange("p g n u e -> p (g n) u e"),
+                    in0=bank[:].bitcast(BF16).rearrange("p u g (n e) -> p (g n) u e", e=2),
+                    in1=row_sign[:, blk]
+                    .rearrange("p g n e -> p (g n) e")
+                    .unsqueeze(2)
+                    .to_broadcast([P, UNIT_PASSES * P, 2, 2]),
+                    op=ALU.mult,
+                )
+            else:
+                i0 = part * UNIT_ROWS - H
+                nc.vector.tensor_tensor(
+                    out=grouped[:],
+                    in0=bank[:].bitcast(BF16).rearrange("p u g (n e) -> p g n u e", e=2),
+                    in1=col_sign_of[blk][:, :, i0 : i0 + UNIT_ROWS].rearrange(
+                        "p n (g u e) -> p g n u e", g=UNIT_PASSES, u=2
+                    ),
+                    op=ALU.mult,
+                )
             return grouped
 
         def quantise_x(grouped):
@@ -209,52 +272,90 @@ def tile_bcnnresnet_k_kernel(tc, feat, W, b, out):
             )
             return codes, scales
 
-        def multiply(h, codes, scales, acc):
-            part = h % UNITS_PER_BLOCK
+        acc_of = {}
+        passes_done = [0] * BLOCKS
+
+        def multiply(h, codes, scales):
+            blk, part = divmod(h, UNITS_PER_BLOCK)
+            if passes_done[blk] == 0:
+                acc_of[blk] = acc_pool.tile([P, C], F32, name="acc")
             for g in range(UNIT_PASSES):
                 k_pass = part * UNIT_PASSES + g
                 nc.tensor.matmul_mx(
-                    out=acc[:],
+                    out=acc_of[blk][:],
                     lhsT=codes[:, g, :].bitcast(FP8X4),
                     lhsT_scale=scales[:, g, :],
                     rhs=w_codes[:, k_pass, :].bitcast(FP8X4),
                     rhs_scale=w_scales[:, k_pass, :],
-                    start=(k_pass == 0),
-                    stop=(k_pass == PASSES - 1),
+                    start=(passes_done[blk] == 0),
+                    stop=(passes_done[blk] == PASSES - 1),
                 )
+                passes_done[blk] += 1
 
-        def finish_block(blk, acc):
+        def finish_block(blk):
             result = out_pool.tile([P, C], F32, name="result")
-            nc.vector.tensor_tensor(out=result[:], in0=acc[:], in1=bias_rows[:], op=ALU.add)
+            nc.vector.tensor_tensor(out=result[:], in0=acc_of[blk][:], in1=bias_rows[:], op=ALU.add)
             nc.sync.dma_start(out=out[blk * P : (blk + 1) * P, :], in_=result[:])
 
-        roots_of, bank_of, grouped_of, codes_of, acc_of = {}, {}, {}, {}, {}
-        for step in range(UNITS + 5):
-            w = step + W_UNITS_AHEAD
-            if w < W_UNITS:
-                w_grouped_of[w] = regroup_w(w_bank_of[w])
-            if step < UNITS:
-                roots_of[step] = take_roots(step)
-            h = step - 1
-            if 0 <= h < UNITS:
-                sign_slabs(h, roots_of[h])
-                bank_of[h] = transpose_unit(roots_of[h][:].rearrange("p s d -> p (s d)").bitcast(F32))
-            if w + 1 < W_UNITS:
-                w_bank_of[w + 1] = transpose_w(w + 1)
-            h = step - 5
-            if 0 <= h < UNITS and h % UNITS_PER_BLOCK == UNITS_PER_BLOCK - 1:
-                finish_block(h // UNITS_PER_BLOCK, acc_of[h // UNITS_PER_BLOCK])
-            h = step - 2
-            if 0 <= h < UNITS:
+        unit_at = {}
+        for blk in range(BLOCKS):
+            for k in range(HALF_UNITS):
+                first = blk * UNITS_PER_BLOCK
+                unit_at[k + 1 if blk == 0 else first + HALF_UNITS + k] = first + k
+                unit_at[first + UNITS_PER_BLOCK + k] = first + HALF_UNITS + k
+        w_at = {}
+        for w in range(W_AHEAD, HALF_UNITS):
+            w_at[HALF_UNITS + w - W_AHEAD] = w
+        for k in range(HALF_UNITS):
+            first = (1 if k < HALF_UNITS // 2 else 2) * UNITS_PER_BLOCK + HALF_UNITS
+            w_at[first + 2 * (k % (HALF_UNITS // 2))] = HALF_UNITS + k
+
+        bank_of, grouped_of, codes_of = {}, {}, {}
+        ready_w = W_AHEAD
+        waiting = []
+        finish_soon, finished = [], []
+        for step in range(STEPS + HALF_UNITS + 4):
+            w = w_at.get(step)
+            if w is not None and w >= HALF_UNITS:
+                w_grouped_of[w] = regroup_w(w, w_bank_of[w])
+            if step < STEPS:
+                take_roots(step)
+            if step == 1:
+                for blk in range(2):
+                    load_col_sign(blk)
+            if step in (2 * UNITS_PER_BLOCK, 3 * UNITS_PER_BLOCK):
+                load_col_sign(step // UNITS_PER_BLOCK)
+            if 1 <= step <= STEPS:
+                sign_rows(step - 1)
+            h = unit_at.get(step)
+            if h is not None:
+                bank_of[h] = transpose_x(h)
+            for blk in finish_soon:
+                finish_block(blk)
+            finish_soon = []
+            h = unit_at.get(step - 1)
+            if h is not None:
                 grouped_of[h] = regroup_x(h, bank_of[h])
-            h = step - 3
-            if 0 <= h < UNITS:
+            if w is not None and w < HALF_UNITS:
+                w_grouped_of[w] = regroup_w(w, w_bank_of[w])
+            if w is not None and w + 1 < W_UNITS:
+                w_bank_of[w + 1] = transpose_w(w + 1)
+            h = unit_at.get(step - 2)
+            if h is not None:
                 codes_of[h] = quantise_x(grouped_of[h])
-            if w < W_UNITS:
+                waiting.append(h)
+            w = w_at.get(step - 1)
+            if w is not None:
                 quantise_w(w, w_grouped_of[w])
-            if 0 <= h < UNITS and h % 2 == 1:
-                blk = h // UNITS_PER_BLOCK
-                if h % UNITS_PER_BLOCK == 1:
-                    acc_of[blk] = acc_pool.tile([P, C], F32, name="acc")
-                for unit in (h - 1, h):
-                    multiply(unit, codes_of[unit][0], codes_of[unit][1], acc_of[blk])
+                ready_w = w + 1
+            now = [h for h in waiting if h % UNITS_PER_BLOCK < ready_w]
+            if len(now) >= 2 or step > STEPS + HALF_UNITS:
+                for h in now:
+                    multiply(h, codes_of[h][0], codes_of[h][1])
+                    waiting.remove(h)
+                for blk in range(BLOCKS):
+                    if passes_done[blk] == PASSES and blk not in finished:
+                        finish_soon.append(blk)
+                        finished.append(blk)
+        for blk in finish_soon:
+            finish_block(blk)

@@ -14,7 +14,8 @@ AXIS = mybir.AxisListType
 
 P = 128
 B, D, C = 512, 128, 128
-H = D // 2
+LOW = 96
+HIGH = D - LOW
 EPS_SQRT = 1e-10
 EPS_NORM = 1e-12
 
@@ -24,7 +25,8 @@ PASSES = D * D // K_PASS
 UNIT_PASSES = 2
 UNIT_ROWS = 8
 UNITS_PER_BLOCK = PASSES // UNIT_PASSES
-HALF_UNITS = UNITS_PER_BLOCK // 2
+LOW_UNITS = LOW // UNIT_ROWS
+HIGH_UNITS = HIGH // UNIT_ROWS
 STEPS = BLOCKS * UNITS_PER_BLOCK
 W_UNITS = UNITS_PER_BLOCK
 W_LOADS = 8
@@ -91,7 +93,7 @@ def tile_bcnnresnet_k_kernel(tc, feat, W, b, out):
             per_load = W_UNITS // W_LOADS
             rows = w_rows[w // per_load]
             first = (w % per_load) * UNIT_ROWS * D
-            if w < HALF_UNITS:
+            if w < LOW_UNITS:
                 return transpose_rows(rows[:, first : first + UNIT_ROWS * D].bitcast(F32))
             bank = banks_pool.tile([P, UNIT_PASSES, 4, P], BF16, name="bank")
             for g in range(UNIT_PASSES):
@@ -102,13 +104,10 @@ def tile_bcnnresnet_k_kernel(tc, feat, W, b, out):
 
         def regroup_w(w, bank):
             grouped = grouped_pool.tile([P, UNIT_PASSES, C, 4], BF16, name="w_grouped", align_bytes=64)
-            if w < HALF_UNITS:
+            if w < LOW_UNITS:
                 words_out = grouped[:].rearrange("p g c t -> p (g c) t").bitcast(F32)
                 words_in = bank[:].rearrange("p u g c -> p (g c) u")
-                if w < W_AHEAD:
-                    nc.scalar.copy(out=words_out, in_=words_in)
-                else:
-                    nc.vector.tensor_copy(out=words_out, in_=words_in)
+                nc.scalar.copy(out=words_out, in_=words_in)
             else:
                 nc.scalar.copy(out=grouped[:], in_=bank[:].rearrange("p g t c -> p g c t"))
             return grouped
@@ -169,17 +168,17 @@ def tile_bcnnresnet_k_kernel(tc, feat, W, b, out):
         sign_twice = keep.tile([P, BLOCKS, 2, D], BF16, name="sign_twice")
         nc.vector.tensor_copy(out=sign_twice[:], in_=sign_f32[:].unsqueeze(2).to_broadcast([P, BLOCKS, 2, D]))
 
-        sign_high = keep.tile([P, BLOCKS, H], BF16, name="sign_high")
-        nc.vector.tensor_copy(out=sign_high[:], in_=sign_f32[:, :, H:])
-        words_high = P * H // 2
-        parked = out[(BLOCKS - 1) * P :, :].rearrange("r c -> (r c)")
+        sign_high = keep.tile([P, BLOCKS, HIGH], BF16, name="sign_high")
+        nc.vector.tensor_copy(out=sign_high[:], in_=sign_f32[:, :, LOW:])
+        words_high = P * HIGH // 2
+        parked = out[(BLOCKS - 1) * P : (BLOCKS - 1) * P + BLOCKS * words_high // C, :].rearrange("r c -> (r c)")
         nc.sync.dma_start(
             out=parked.rearrange("(blk n w) -> n blk w", blk=BLOCKS, n=P), in_=sign_high[:].bitcast(F32)
         )
         col_sign_of = {}
 
         def load_col_sign(blk):
-            col_sign = col_sign_pool.tile([P, P, H], BF16, name="col_sign")
+            col_sign = col_sign_pool.tile([P, P, HIGH], BF16, name="col_sign")
             nc.sync.dma_start(
                 out=col_sign[:].rearrange("p n i -> p (n i)").bitcast(F32),
                 in_=parked[blk * words_high : (blk + 1) * words_high].partition_broadcast(P),
@@ -206,7 +205,7 @@ def tile_bcnnresnet_k_kernel(tc, feat, W, b, out):
         table_of = {}
 
         def columns_from(i):
-            return 0 if i < H else H
+            return 0 if i < LOW else LOW
 
         def take_roots(step):
             blk, part = divmod(step, UNITS_PER_BLOCK)
@@ -231,7 +230,7 @@ def tile_bcnnresnet_k_kernel(tc, feat, W, b, out):
         def transpose_x(h):
             blk, part = divmod(h, UNITS_PER_BLOCK)
             i0 = part * UNIT_ROWS
-            if part < HALF_UNITS:
+            if part < LOW_UNITS:
                 return transpose_rows(
                     table_of[blk][:, i0 : i0 + UNIT_ROWS, :].rearrange("p s d -> p (s d)").bitcast(F32)
                 )
@@ -240,7 +239,7 @@ def tile_bcnnresnet_k_kernel(tc, feat, W, b, out):
         def regroup_x(h, bank):
             blk, part = divmod(h, UNITS_PER_BLOCK)
             grouped = grouped_pool.tile([P, UNIT_PASSES, P, 2, 2], BF16, name="grouped", align_bytes=64)
-            if part < HALF_UNITS:
+            if part < LOW_UNITS:
                 nc.vector.tensor_tensor(
                     out=grouped[:].rearrange("p g n u e -> p (g n) u e"),
                     in0=bank[:].bitcast(BF16).rearrange("p u g (n e) -> p (g n) u e", e=2),
@@ -251,7 +250,7 @@ def tile_bcnnresnet_k_kernel(tc, feat, W, b, out):
                     op=ALU.mult,
                 )
             else:
-                i0 = part * UNIT_ROWS - H
+                i0 = part * UNIT_ROWS - LOW
                 nc.vector.tensor_tensor(
                     out=grouped[:],
                     in0=bank[:].bitcast(BF16).rearrange("p u g (n e) -> p g n u e", e=2),
@@ -299,24 +298,24 @@ def tile_bcnnresnet_k_kernel(tc, feat, W, b, out):
 
         unit_at = {}
         for blk in range(BLOCKS):
-            for k in range(HALF_UNITS):
-                first = blk * UNITS_PER_BLOCK
-                unit_at[k + 1 if blk == 0 else first + HALF_UNITS + k] = first + k
-                unit_at[first + UNITS_PER_BLOCK + k] = first + HALF_UNITS + k
+            first = blk * UNITS_PER_BLOCK
+            for k in range(LOW_UNITS):
+                unit_at[first + 1 + k + k // (4 if blk == 0 else 3)] = first + k
+            for k in range(HIGH_UNITS):
+                unit_at[first + UNITS_PER_BLOCK + (4 * k if blk < BLOCKS - 1 else k)] = first + LOW_UNITS + k
         w_at = {}
-        for w in range(W_AHEAD, HALF_UNITS):
-            w_at[HALF_UNITS + w - W_AHEAD] = w
-        for k in range(HALF_UNITS):
-            first = (1 if k < HALF_UNITS // 2 else 2) * UNITS_PER_BLOCK + HALF_UNITS
-            w_at[first + 2 * (k % (HALF_UNITS // 2))] = HALF_UNITS + k
+        for w in range(W_AHEAD, LOW_UNITS):
+            w_at[w - W_AHEAD] = w
+        for w in range(LOW_UNITS, W_UNITS):
+            w_at[UNITS_PER_BLOCK + w] = w
 
         bank_of, grouped_of, codes_of = {}, {}, {}
         ready_w = W_AHEAD
         waiting = []
         finish_soon, finished = [], []
-        for step in range(STEPS + HALF_UNITS + 4):
+        for step in range(STEPS + HIGH_UNITS + 4):
             w = w_at.get(step)
-            if w is not None and w >= HALF_UNITS:
+            if w is not None:
                 w_grouped_of[w] = regroup_w(w, w_bank_of[w])
             if step < STEPS:
                 take_roots(step)
@@ -336,10 +335,8 @@ def tile_bcnnresnet_k_kernel(tc, feat, W, b, out):
             h = unit_at.get(step - 1)
             if h is not None:
                 grouped_of[h] = regroup_x(h, bank_of[h])
-            if w is not None and w < HALF_UNITS:
-                w_grouped_of[w] = regroup_w(w, w_bank_of[w])
-            if w is not None and w + 1 < W_UNITS:
-                w_bank_of[w + 1] = transpose_w(w + 1)
+            if step + 1 in w_at:
+                w_bank_of[w_at[step + 1]] = transpose_w(w_at[step + 1])
             h = unit_at.get(step - 2)
             if h is not None:
                 codes_of[h] = quantise_x(grouped_of[h])
@@ -349,7 +346,7 @@ def tile_bcnnresnet_k_kernel(tc, feat, W, b, out):
                 quantise_w(w, w_grouped_of[w])
                 ready_w = w + 1
             now = [h for h in waiting if h % UNITS_PER_BLOCK < ready_w]
-            if len(now) >= 2 or step > STEPS + HALF_UNITS:
+            if len(now) >= 4 or step > STEPS + HIGH_UNITS:
                 for h in now:
                     multiply(h, codes_of[h][0], codes_of[h][1])
                     waiting.remove(h)

@@ -30,7 +30,16 @@ HIGH_UNITS = HIGH // UNIT_ROWS
 STEPS = BLOCKS * UNITS_PER_BLOCK
 W_UNITS = UNITS_PER_BLOCK
 W_LOADS = 8
-W_AHEAD = 3
+SCALAR_ROWS = [0] * 64
+MM_UNITS = 3
+W_AT = {w: w for w in range(12)} | {16 + w: w for w in range(12, 16)}
+
+
+def LAG(step):
+    return 1 if step < 16 else 2
+
+
+W_AHEAD = 2
 
 FLOPS = 2 * B * D * D * C
 
@@ -46,8 +55,8 @@ def tile_bcnnresnet_k_kernel(tc, feat, W, b, out):
         grouped_pool = ctx.enter_context(tc.tile_pool(name="grouped_pool", bufs=4))
         codes_pool = ctx.enter_context(tc.tile_pool(name="codes_pool", bufs=20))
         out_pool = ctx.enter_context(tc.tile_pool(name="out_pool", bufs=2))
-        banks_pool = ctx.enter_context(tc.psum_pool(name="banks_pool", bufs=5))
-        acc_pool = ctx.enter_context(tc.psum_pool(name="acc_pool", bufs=3))
+        banks_pool = ctx.enter_context(tc.psum_pool(name="banks_pool", bufs=6))
+        acc_pool = ctx.enter_context(tc.psum_pool(name="acc_pool", bufs=2))
 
         feat_sb = keep.tile([P, BLOCKS, D], BF16, name="feat_sb")
         nc.sync.dma_start(out=feat_sb[:], in_=feat.rearrange("(blk p) d -> p blk d", p=P))
@@ -126,28 +135,29 @@ def tile_bcnnresnet_k_kernel(tc, feat, W, b, out):
             nc.scalar.activation(
                 out=mag[:, blk, :], in_=feat_sb[:, blk, :], func=FUNC.Abs, accum_out=sum_mag[:, blk : blk + 1]
             )
-        w_bank_of, w_grouped_of = {}, {}
-        for w in range(W_AHEAD):
-            w_bank_of[w] = transpose_w(w)
-            w_grouped_of[w] = regroup_w(w, w_bank_of[w])
-        w_bank_of[W_AHEAD] = transpose_w(W_AHEAD)
 
         nonzero = keep.tile([P, BLOCKS, D], BF16, name="nonzero")
         nc.vector.tensor_single_scalar(out=nonzero[:], in_=feat_sb[:], scalar=0.0, op=ALU.not_equal)
+        negative = keep.tile([P, BLOCKS, D], BF16, name="negative")
+        nc.vector.tensor_single_scalar(out=negative[:], in_=feat_sb[:], scalar=0.0, op=ALU.is_lt)
         count = keep.tile([P, BLOCKS], F32, name="count")
         nc.vector.tensor_reduce(out=count[:], in_=nonzero[:], axis=AXIS.X, op=ALU.add)
-        count_sq = keep.tile([P, BLOCKS], F32, name="count_sq")
-        nc.vector.tensor_tensor(out=count_sq[:], in0=count[:], in1=count[:], op=ALU.mult)
+        sign_f32 = keep.tile([P, BLOCKS, D], F32, name="sign_f32")
+        nc.vector.scalar_tensor_tensor(
+            out=sign_f32[:, 0], in0=feat_sb[:, 0], scalar=0.0, in1=negative[:, 0], op0=ALU.is_gt, op1=ALU.subtract
+        )
+        eps_count = keep.tile([P, BLOCKS], F32, name="eps_count")
+        nc.vector.scalar_tensor_tensor(
+            out=eps_count[:], in0=count[:], scalar=EPS_SQRT, in1=count[:], op0=ALU.mult, op1=ALU.mult
+        )
         sum_sq = keep.tile([P, BLOCKS], F32, name="sum_sq")
         nc.vector.tensor_tensor(out=sum_sq[:], in0=sum_mag[:], in1=sum_mag[:], op=ALU.mult)
         norm_sq = keep.tile([P, BLOCKS], F32, name="norm_sq")
         nc.vector.scalar_tensor_tensor(
-            out=norm_sq[:], in0=count_sq[:], scalar=EPS_SQRT, in1=sum_sq[:], op0=ALU.mult, op1=ALU.add
+            out=norm_sq[:], in0=eps_count[:], scalar=EPS_NORM * EPS_NORM, in1=sum_sq[:], op0=ALU.max, op1=ALU.add
         )
-        clamped = keep.tile([P, BLOCKS], F32, name="clamped")
-        nc.vector.tensor_scalar_max(out=clamped[:], in0=norm_sq[:], scalar1=EPS_NORM * EPS_NORM)
         inv_norm_sq = keep.tile([P, BLOCKS], F32, name="inv_norm_sq")
-        nc.vector.reciprocal(out=inv_norm_sq[:], in_=clamped[:])
+        nc.vector.reciprocal(out=inv_norm_sq[:], in_=norm_sq[:])
         row_scale = keep.tile([P, BLOCKS, D], F32, name="row_scale")
 
         def scale_block(blk):
@@ -159,22 +169,47 @@ def tile_bcnnresnet_k_kernel(tc, feat, W, b, out):
         eps_scaled = keep.tile([P, BLOCKS], F32, name="eps_scaled")
         nc.vector.tensor_scalar_mul(out=eps_scaled[:], in0=inv_norm_sq[:], scalar1=EPS_SQRT)
 
-        negative = keep.tile([P, BLOCKS, D], BF16, name="negative")
-        nc.vector.tensor_single_scalar(out=negative[:], in_=feat_sb[:], scalar=0.0, op=ALU.is_lt)
-        sign_f32 = keep.tile([P, BLOCKS, D], F32, name="sign_f32")
-        nc.vector.scalar_tensor_tensor(
-            out=sign_f32[:], in0=feat_sb[:], scalar=0.0, in1=negative[:], op0=ALU.is_gt, op1=ALU.subtract
-        )
         sign_twice = keep.tile([P, BLOCKS, 2, D], BF16, name="sign_twice")
-        nc.vector.tensor_copy(out=sign_twice[:], in_=sign_f32[:].unsqueeze(2).to_broadcast([P, BLOCKS, 2, D]))
+        nc.vector.tensor_copy(out=sign_twice[:, 0], in_=sign_f32[:, 0].unsqueeze(1).to_broadcast([P, 2, D]))
+        nc.vector.scalar_tensor_tensor(
+            out=sign_f32[:, 1:], in0=feat_sb[:, 1:], scalar=0.0, in1=negative[:, 1:], op0=ALU.is_gt, op1=ALU.subtract
+        )
+
+        w_bank_of, w_grouped_of = {}, {}
+        for w in range(W_AHEAD):
+            w_bank_of[w] = transpose_w(w)
+        row_sign = keep.tile([P, BLOCKS, UNIT_PASSES, P, 2], BF16, name="row_sign")
+
+        def spread_row_sign(blk):
+            bank = banks_pool.tile([P, P], F32, name="bank")
+            nc.tensor.transpose(
+                out=bank[:], in_=sign_twice[:, blk].rearrange("p h d -> p (h d)").bitcast(F32), identity=ident[:]
+            )
+            nc.vector.tensor_copy(
+                out=row_sign[:, blk].rearrange("p g n e -> p g (n e)").bitcast(F32),
+                in_=bank[:].unsqueeze(1).to_broadcast([P, UNIT_PASSES, P]),
+            )
 
         sign_high = keep.tile([P, BLOCKS, HIGH], BF16, name="sign_high")
-        nc.vector.tensor_copy(out=sign_high[:], in_=sign_f32[:, :, LOW:])
         words_high = P * HIGH // 2
         parked = out[(BLOCKS - 1) * P : (BLOCKS - 1) * P + BLOCKS * words_high // C, :].rearrange("r c -> (r c)")
-        nc.sync.dma_start(
-            out=parked.rearrange("(blk n w) -> n blk w", blk=BLOCKS, n=P), in_=sign_high[:].bitcast(F32)
-        )
+
+        sign_pairs = keep.tile([P, BLOCKS, HIGH, 2], BF16, name="sign_pairs")
+
+        def park_signs():
+            nc.vector.tensor_copy(out=sign_high[:], in_=sign_f32[:, :, LOW:])
+            nc.gpsimd.tensor_scalar(
+                out=sign_pairs[:],
+                in0=sign_f32[:, :, LOW:].unsqueeze(3).to_broadcast([P, BLOCKS, HIGH, 2]),
+                scalar1=1.0,
+                scalar2=0.0,
+                op0=ALU.mult,
+                op1=ALU.add,
+            )
+            nc.sync.dma_start(
+                out=parked.rearrange("(blk n w) -> n blk w", blk=BLOCKS, n=P), in_=sign_high[:].bitcast(F32)
+            )
+
         col_sign_of = {}
 
         def load_col_sign(blk):
@@ -184,23 +219,6 @@ def tile_bcnnresnet_k_kernel(tc, feat, W, b, out):
                 in_=parked[blk * words_high : (blk + 1) * words_high].partition_broadcast(P),
             )
             col_sign_of[blk] = col_sign
-
-        sign_bank = banks_pool.tile([P, BLOCKS, P], F32, name="bank")
-        for blk in range(BLOCKS):
-            nc.tensor.transpose(
-                out=sign_bank[:, blk, :],
-                in_=sign_twice[:, blk].rearrange("p h d -> p (h d)").bitcast(F32),
-                identity=ident[:],
-            )
-        row_sign = keep.tile([P, BLOCKS, UNIT_PASSES, P, 2], BF16, name="row_sign")
-        nc.vector.tensor_copy(
-            out=row_sign[:].rearrange("p blk g n e -> p blk g (n e)").bitcast(F32),
-            in_=sign_bank[:].unsqueeze(2).to_broadcast([P, BLOCKS, UNIT_PASSES, P]),
-        )
-        for blk in range(1, BLOCKS):
-            scale_block(blk)
-        for w in range(W_AHEAD):
-            quantise_w(w, w_grouped_of[w])
 
         table_of = {}
 
@@ -221,11 +239,33 @@ def tile_bcnnresnet_k_kernel(tc, feat, W, b, out):
                     bias=eps_scaled[:, blk : blk + 1],
                 )
 
-        def sign_rows(step):
+        def scalar_signs(step):
             blk, part = divmod(step, UNITS_PER_BLOCK)
+            rows = range(part * UNIT_ROWS, (part + 1) * UNIT_ROWS)
+            return rows[: SCALAR_ROWS[step]]
+
+        def sign_rows(step, on_scalar):
+            blk, part = divmod(step, UNITS_PER_BLOCK)
+            if part >= LOW_UNITS:
+                if not on_scalar:
+                    rows = slice(part * UNIT_ROWS, (part + 1) * UNIT_ROWS)
+                    short = table_of[blk][:, rows, LOW:].rearrange("p s (w e) -> p s w e", e=2)
+                    factors = sign_pairs[:, blk, part * UNIT_ROWS - LOW : (part + 1) * UNIT_ROWS - LOW, :]
+                    nc.vector.tensor_tensor(
+                        out=short,
+                        in0=short,
+                        in1=factors.unsqueeze(2).to_broadcast([P, UNIT_ROWS, HIGH // 2, 2]),
+                        op=ALU.mult,
+                    )
+                return
             for i in range(part * UNIT_ROWS, (part + 1) * UNIT_ROWS):
-                row = table_of[blk][:, i, columns_from(i) :]
-                nc.vector.tensor_scalar_mul(out=row, in0=row, scalar1=sign_f32[:, blk, i : i + 1])
+                if (i in scalar_signs(step)) == on_scalar:
+                    row = table_of[blk][:, i, columns_from(i) :]
+                    factor = sign_f32[:, blk, i : i + 1]
+                    if on_scalar:
+                        nc.scalar.activation(out=row, in_=row, func=FUNC.Copy, scale=factor)
+                    else:
+                        nc.vector.tensor_scalar_mul(out=row, in0=row, scalar1=factor)
 
         def transpose_x(h):
             blk, part = divmod(h, UNITS_PER_BLOCK)
@@ -296,49 +336,76 @@ def tile_bcnnresnet_k_kernel(tc, feat, W, b, out):
             nc.vector.tensor_tensor(out=result[:], in0=acc_of[blk][:], in1=bias_rows[:], op=ALU.add)
             nc.sync.dma_start(out=out[blk * P : (blk + 1) * P, :], in_=result[:])
 
+        order = []
+        for blk in range(BLOCKS + 1):
+            low = [blk * UNITS_PER_BLOCK + k for k in range(LOW_UNITS)] if blk < BLOCKS else []
+            high = [(blk - 1) * UNITS_PER_BLOCK + LOW_UNITS + k for k in range(HIGH_UNITS)] if blk > 0 else []
+            if blk == BLOCKS:
+                order += high
+            else:
+                for k in range(LOW_UNITS):
+                    if k % 3 == 0 and high:
+                        order.append(high.pop(0))
+                    order.append(low[k])
         unit_at = {}
-        for blk in range(BLOCKS):
-            first = blk * UNITS_PER_BLOCK
-            for k in range(LOW_UNITS):
-                unit_at[first + 1 + k + k // (4 if blk == 0 else 3)] = first + k
-            for k in range(HIGH_UNITS):
-                unit_at[first + UNITS_PER_BLOCK + (4 * k if blk < BLOCKS - 1 else k)] = first + LOW_UNITS + k
-        w_at = {}
-        for w in range(W_AHEAD, LOW_UNITS):
-            w_at[w - W_AHEAD] = w
-        for w in range(LOW_UNITS, W_UNITS):
-            w_at[UNITS_PER_BLOCK + w] = w
-
+        step = 0
+        for h in order:
+            blk, part = divmod(h, UNITS_PER_BLOCK)
+            step = max(step + 1, blk * UNITS_PER_BLOCK + 1 + part if part < LOW_UNITS else (blk + 1) * UNITS_PER_BLOCK)
+            unit_at[step] = h
+        last_step = step
+        w_at = W_AT
         bank_of, grouped_of, codes_of = {}, {}, {}
-        ready_w = W_AHEAD
+        ready_w = 0
         waiting = []
-        finish_soon, finished = [], []
-        for step in range(STEPS + HIGH_UNITS + 4):
+        finish_at, finished = {}, []
+        transposed, copied, quantised = [], [], []
+        for step in range(last_step + 7):
             w = w_at.get(step)
             if w is not None:
+                if w not in w_bank_of:
+                    w_bank_of[w] = transpose_w(w)
                 w_grouped_of[w] = regroup_w(w, w_bank_of[w])
             if step < STEPS:
                 take_roots(step)
-            if step == 1:
+            if 1 <= step <= STEPS:
+                sign_rows(step - 1, True)
+            if step == 2:
                 for blk in range(2):
                     load_col_sign(blk)
-            if step in (2 * UNITS_PER_BLOCK, 3 * UNITS_PER_BLOCK):
+            if step in (2 * UNITS_PER_BLOCK + 2, 3 * UNITS_PER_BLOCK + 2):
                 load_col_sign(step // UNITS_PER_BLOCK)
             if 1 <= step <= STEPS:
-                sign_rows(step - 1)
+                sign_rows(step - 1, False)
+            if step == 0:
+                spread_row_sign(0)
+                park_signs()
+            if step == 1:
+                nc.gpsimd.tensor_scalar(
+                    out=sign_twice[:, 1:],
+                    in0=sign_f32[:, 1:].unsqueeze(2).to_broadcast([P, BLOCKS - 1, 2, D]),
+                    scalar1=1.0,
+                    scalar2=0.0,
+                    op0=ALU.mult,
+                    op1=ALU.add,
+                )
+            if step in (4, 5, 6):
+                scale_block(step - 3)
+                spread_row_sign(step - 3)
             h = unit_at.get(step)
             if h is not None:
                 bank_of[h] = transpose_x(h)
-            for blk in finish_soon:
-                finish_block(blk)
-            finish_soon = []
-            h = unit_at.get(step - 1)
-            if h is not None:
-                grouped_of[h] = regroup_x(h, bank_of[h])
-            if step + 1 in w_at:
+                transposed.append((step, h))
+            if step + 1 in w_at and w_at[step + 1] not in w_bank_of:
                 w_bank_of[w_at[step + 1]] = transpose_w(w_at[step + 1])
-            h = unit_at.get(step - 2)
-            if h is not None:
+            for blk in finish_at.get(step, []):
+                finish_block(blk)
+            if transposed and transposed[0][0] <= step - LAG(transposed[0][0]):
+                h = transposed.pop(0)[1]
+                grouped_of[h] = regroup_x(h, bank_of[h])
+                copied.append((step, h))
+            if copied and copied[0][0] < step:
+                h = copied.pop(0)[1]
                 codes_of[h] = quantise_x(grouped_of[h])
                 waiting.append(h)
             w = w_at.get(step - 1)
@@ -346,13 +413,15 @@ def tile_bcnnresnet_k_kernel(tc, feat, W, b, out):
                 quantise_w(w, w_grouped_of[w])
                 ready_w = w + 1
             now = [h for h in waiting if h % UNITS_PER_BLOCK < ready_w]
-            if len(now) >= 4 or step > STEPS + HIGH_UNITS:
+            if len(now) >= MM_UNITS or step > last_step + 1:
                 for h in now:
                     multiply(h, codes_of[h][0], codes_of[h][1])
                     waiting.remove(h)
                 for blk in range(BLOCKS):
                     if passes_done[blk] == PASSES and blk not in finished:
-                        finish_soon.append(blk)
+                        finish_at.setdefault(step + 2 if step < last_step else step + 1, []).append(blk)
                         finished.append(blk)
-        for blk in finish_soon:
-            finish_block(blk)
+        for later in sorted(finish_at):
+            if later >= last_step + 7:
+                for blk in finish_at[later]:
+                    finish_block(blk)

@@ -370,7 +370,7 @@ def tile_bcnnresnet_k_kernel(tc, feat, W, b, out):
                 take_roots(step)
             if 1 <= step <= STEPS:
                 sign_rows(step - 1, True)
-            if step == 2:
+            if step == 8:
                 for blk in range(2):
                     load_col_sign(blk)
             if step in (2 * UNITS_PER_BLOCK + 2, 3 * UNITS_PER_BLOCK + 2):
@@ -379,6 +379,7 @@ def tile_bcnnresnet_k_kernel(tc, feat, W, b, out):
                 sign_rows(step - 1, False)
             if step == 0:
                 spread_row_sign(0)
+            if step == 7:
                 park_signs()
             if step == 1:
                 nc.gpsimd.tensor_scalar(

@@ -28,18 +28,24 @@ UNITS_PER_BLOCK = PASSES // UNIT_PASSES
 LOW_UNITS = LOW // UNIT_ROWS
 HIGH_UNITS = HIGH // UNIT_ROWS
 STEPS = BLOCKS * UNITS_PER_BLOCK
-W_UNITS = UNITS_PER_BLOCK
 W_LOADS = 8
-SCALAR_ROWS = [0] * 64
-MM_UNITS = 3
-W_AT = {w: w for w in range(12)} | {16 + w: w for w in range(12, 16)}
-
-
-def LAG(step):
-    return 1 if step < 16 else 2
-
-
-W_AHEAD = 2
+GAP = 3
+HPER = 2
+HA = 28
+HN = 8
+HB = 34
+WA = 12
+WB = 12
+WS = 1
+WV = 99
+GP_ROWS = 0
+SC_ROWS = (0, 0, 0, 0)
+MM_UNITS = 4
+X_BANKS = 4
+W_BANKS = 1
+ACCS = 3
+HIGH_TURN = [HA + j // HPER if j < HN else HB + (j - HN) // HPER for j in range(4 * HIGH_UNITS // 2)]
+W_ROUNDS = [w if w < WA else WB + WS * (w - WA) for w in range(LOW_UNITS)]
 
 FLOPS = 2 * B * D * D * C
 
@@ -50,13 +56,15 @@ def tile_bcnnresnet_k_kernel(tc, feat, W, b, out):
         ctx.enter_context(tc.manual_schedule())
         keep = ctx.enter_context(tc.tile_pool(name="keep", bufs=1))
         w_in = ctx.enter_context(tc.tile_pool(name="w_in", bufs=W_LOADS))
+        raw_pool = ctx.enter_context(tc.tile_pool(name="raw_pool", bufs=4))
         table_pool = ctx.enter_context(tc.tile_pool(name="table_pool", bufs=2))
         col_sign_pool = ctx.enter_context(tc.tile_pool(name="col_sign_pool", bufs=2))
-        grouped_pool = ctx.enter_context(tc.tile_pool(name="grouped_pool", bufs=4))
-        codes_pool = ctx.enter_context(tc.tile_pool(name="codes_pool", bufs=20))
+        grouped_pool = ctx.enter_context(tc.tile_pool(name="grouped_pool", bufs=3))
+        codes_pool = ctx.enter_context(tc.tile_pool(name="codes_pool", bufs=10))
         out_pool = ctx.enter_context(tc.tile_pool(name="out_pool", bufs=2))
-        banks_pool = ctx.enter_context(tc.psum_pool(name="banks_pool", bufs=6))
-        acc_pool = ctx.enter_context(tc.psum_pool(name="acc_pool", bufs=2))
+        banks_pool = ctx.enter_context(tc.psum_pool(name="banks_pool", bufs=X_BANKS))
+        w_bank_pool = ctx.enter_context(tc.psum_pool(name="w_bank_pool", bufs=W_BANKS))
+        acc_pool = ctx.enter_context(tc.psum_pool(name="acc_pool", bufs=ACCS))
 
         feat_sb = keep.tile([P, BLOCKS, D], BF16, name="feat_sb")
         nc.sync.dma_start(out=feat_sb[:], in_=feat.rearrange("(blk p) d -> p blk d", p=P))
@@ -82,8 +90,8 @@ def tile_bcnnresnet_k_kernel(tc, feat, W, b, out):
         w_codes = keep.tile([P, PASSES, C], U32, name="w_codes", align_bytes=64)
         w_scales = keep.tile([P, PASSES, C], U8, name="w_scales", align_bytes=64)
 
-        def transpose_rows(words):
-            bank = banks_pool.tile([P, 2, UNIT_PASSES, P], F32, name="bank")
+        def transpose_rows(words, pool):
+            bank = pool.tile([P, 2, UNIT_PASSES, P], F32, name="bank")
             for g in range(UNIT_PASSES):
                 for u in range(2):
                     first = (2 * g + u) * P
@@ -98,34 +106,40 @@ def tile_bcnnresnet_k_kernel(tc, feat, W, b, out):
                     nc.tensor.transpose(out=bank[:, u, g, :], in_=words[:, :, i0 // 2 + 2 * g + u], identity=ident[:])
             return bank
 
-        def transpose_w(w):
-            per_load = W_UNITS // W_LOADS
-            rows = w_rows[w // per_load]
+        def turn_w_rows(w):
+            per_load = UNITS_PER_BLOCK // W_LOADS
             first = (w % per_load) * UNIT_ROWS * D
-            if w < LOW_UNITS:
-                return transpose_rows(rows[:, first : first + UNIT_ROWS * D].bitcast(F32))
-            bank = banks_pool.tile([P, UNIT_PASSES, 4, P], BF16, name="bank")
-            for g in range(UNIT_PASSES):
-                for t in range(4):
-                    at = first + (4 * g + t) * D
-                    nc.tensor.transpose(out=bank[:, g, t, :], in_=rows[:, at : at + D], identity=ident_bf[:])
-            return bank
+            return transpose_rows(w_rows[w // per_load][:, first : first + UNIT_ROWS * D].bitcast(F32), w_bank_pool)
 
-        def regroup_w(w, bank):
+        def copy_w_rows(w, bank):
             grouped = grouped_pool.tile([P, UNIT_PASSES, C, 4], BF16, name="w_grouped", align_bytes=64)
-            if w < LOW_UNITS:
-                words_out = grouped[:].rearrange("p g c t -> p (g c) t").bitcast(F32)
-                words_in = bank[:].rearrange("p u g c -> p (g c) u")
+            words_out = grouped[:].rearrange("p g c t -> p (g c) t").bitcast(F32)
+            words_in = bank[:].rearrange("p u g c -> p (g c) u")
+            if w < WV:
                 nc.scalar.copy(out=words_out, in_=words_in)
             else:
-                nc.scalar.copy(out=grouped[:], in_=bank[:].rearrange("p g t c -> p g c t"))
+                nc.vector.tensor_copy(out=words_out, in_=words_in)
             return grouped
 
-        def quantise_w(w, grouped):
-            passes = slice(w * UNIT_PASSES, (w + 1) * UNIT_PASSES)
+        def turn_w_high(k_pass):
+            passes_per_load = PASSES // W_LOADS
+            rows = w_rows[k_pass // passes_per_load]
+            bank = w_bank_pool.tile([P, P, 4], F32, name="bank")
+            for t in range(4):
+                at = (k_pass % passes_per_load) * K_PASS + t * D
+                nc.tensor.matmul(out=bank[:, :, t], lhsT=rows[:, at : at + D], rhs=ident_bf[:], start=True, stop=True)
+            return bank
+
+        def copy_w_high(bank):
+            grouped = grouped_pool.tile([P, 1, C, 4], BF16, name="w_grouped", align_bytes=64)
+            nc.scalar.copy(out=grouped[:, 0], in_=bank[:])
+            return grouped
+
+        def quantise_w(k_pass, passes, grouped):
+            span = slice(k_pass, k_pass + passes)
             nc.vector.quantize_mx(
-                out=w_codes[:, passes, :].rearrange("p g c -> p (g c)").bitcast(FP8X4),
-                scales=w_scales[:, passes, :].rearrange("p g c -> p (g c)"),
+                out=w_codes[:, span, :].rearrange("p g c -> p (g c)").bitcast(FP8X4),
+                scales=w_scales[:, span, :].rearrange("p g c -> p (g c)"),
                 in_=grouped[:].rearrange("p g c t -> p (g c t)"),
             )
 
@@ -176,8 +190,7 @@ def tile_bcnnresnet_k_kernel(tc, feat, W, b, out):
         )
 
         w_bank_of, w_grouped_of = {}, {}
-        for w in range(W_AHEAD):
-            w_bank_of[w] = transpose_w(w)
+        w_bank_of[0] = turn_w_rows(0)
         row_sign = keep.tile([P, BLOCKS, UNIT_PASSES, P, 2], BF16, name="row_sign")
 
         def spread_row_sign(blk):
@@ -220,68 +233,79 @@ def tile_bcnnresnet_k_kernel(tc, feat, W, b, out):
             )
             col_sign_of[blk] = col_sign
 
-        table_of = {}
+        table_of, raw_of = {}, {}
 
-        def columns_from(i):
-            return 0 if i < LOW else LOW
-
-        def take_roots(step):
-            blk, part = divmod(step, UNITS_PER_BLOCK)
+        def take_roots(units):
+            blk, part = divmod(units[0], UNITS_PER_BLOCK)
             if part == 0:
                 table_of[blk] = table_pool.tile([P, D, D], BF16, name="table")
-            for i in range(part * UNIT_ROWS, (part + 1) * UNIT_ROWS):
-                j0 = columns_from(i)
+            rows = range(part * UNIT_ROWS, (part + len(units)) * UNIT_ROWS)
+            if rows[0] < LOW:
+                raw_of[units[0]] = raw_pool.tile([P, 2 * UNIT_ROWS, D], BF16, name="raw")
+            for i in rows:
                 nc.scalar.activation(
-                    out=table_of[blk][:, i, j0:],
-                    in_=mag[:, blk, j0:],
+                    out=raw_of[units[0]][:, i - rows[0], :] if i < LOW else table_of[blk][:, i, LOW:],
+                    in_=mag[:, blk, :] if i < LOW else mag[:, blk, LOW:],
                     func=FUNC.Sqrt,
                     scale=row_scale[:, blk, i : i + 1],
                     bias=eps_scaled[:, blk : blk + 1],
                 )
 
-        def scalar_signs(step):
-            blk, part = divmod(step, UNITS_PER_BLOCK)
-            rows = range(part * UNIT_ROWS, (part + 1) * UNIT_ROWS)
-            return rows[: SCALAR_ROWS[step]]
+        def sign_short_rows(units):
+            blk, part = divmod(units[0], UNITS_PER_BLOCK)
+            rows = slice(part * UNIT_ROWS, (part + len(units)) * UNIT_ROWS)
+            count = len(units) * UNIT_ROWS
+            short = table_of[blk][:, rows, LOW:].rearrange("p s (w e) -> p s w e", e=2)
+            factors = sign_pairs[:, blk, rows.start - LOW : rows.stop - LOW, :]
+            nc.vector.tensor_tensor(
+                out=short,
+                in0=short,
+                in1=factors.unsqueeze(2).to_broadcast([P, count, HIGH // 2, 2]),
+                op=ALU.mult,
+            )
 
-        def sign_rows(step, on_scalar):
-            blk, part = divmod(step, UNITS_PER_BLOCK)
-            if part >= LOW_UNITS:
-                if not on_scalar:
-                    rows = slice(part * UNIT_ROWS, (part + 1) * UNIT_ROWS)
-                    short = table_of[blk][:, rows, LOW:].rearrange("p s (w e) -> p s w e", e=2)
-                    factors = sign_pairs[:, blk, part * UNIT_ROWS - LOW : (part + 1) * UNIT_ROWS - LOW, :]
-                    nc.vector.tensor_tensor(
-                        out=short,
-                        in0=short,
-                        in1=factors.unsqueeze(2).to_broadcast([P, UNIT_ROWS, HIGH // 2, 2]),
-                        op=ALU.mult,
-                    )
-                return
-            for i in range(part * UNIT_ROWS, (part + 1) * UNIT_ROWS):
-                if (i in scalar_signs(step)) == on_scalar:
-                    row = table_of[blk][:, i, columns_from(i) :]
-                    factor = sign_f32[:, blk, i : i + 1]
-                    if on_scalar:
-                        nc.scalar.activation(out=row, in_=row, func=FUNC.Copy, scale=factor)
-                    else:
-                        nc.vector.tensor_scalar_mul(out=row, in0=row, scalar1=factor)
+        def sign_rows(units, by_scalar, by_gpsimd):
+            blk, part = divmod(units[0], UNITS_PER_BLOCK)
+            first = part * UNIT_ROWS
+            count = len(units) * UNIT_ROWS
+            raw = raw_of[units[0]][:].rearrange("p s d -> p (s d)")
+            table = table_of[blk][:, first : first + count, :].rearrange("p s d -> p (s d)")
+            for s in range(by_scalar):
+                nc.scalar.activation(
+                    out=table[:, s * D : (s + 1) * D],
+                    in_=raw[:, s * D : (s + 1) * D],
+                    func=FUNC.Copy,
+                    scale=sign_f32[:, blk, first + s : first + s + 1],
+                )
+            for s in range(by_scalar, count - by_gpsimd):
+                span = slice(s * D, (s + 1) * D + (2 if by_gpsimd and s == count - by_gpsimd - 1 else 0))
+                nc.vector.tensor_scalar_mul(
+                    out=table[:, span], in0=raw[:, span], scalar1=sign_f32[:, blk, first + s : first + s + 1]
+                )
+            for s in range(count - by_gpsimd, count):
+                nc.gpsimd.tensor_scalar(
+                    out=table[:, s * D : (s + 1) * D],
+                    in0=raw[:, s * D : (s + 1) * D],
+                    scalar1=sign_f32[:, blk, first + s : first + s + 1],
+                    scalar2=0.0,
+                    op0=ALU.mult,
+                    op1=ALU.add,
+                )
 
         def transpose_x(h):
             blk, part = divmod(h, UNITS_PER_BLOCK)
             i0 = part * UNIT_ROWS
             if part < LOW_UNITS:
                 return transpose_rows(
-                    table_of[blk][:, i0 : i0 + UNIT_ROWS, :].rearrange("p s d -> p (s d)").bitcast(F32)
+                    table_of[blk][:, i0 : i0 + UNIT_ROWS, :].rearrange("p s d -> p (s d)").bitcast(F32), banks_pool
                 )
             return transpose_cols(table_of[blk], i0)
 
-        def regroup_x(h, bank):
+        def regroup_x(h, bank, grouped):
             blk, part = divmod(h, UNITS_PER_BLOCK)
-            grouped = grouped_pool.tile([P, UNIT_PASSES, P, 2, 2], BF16, name="grouped", align_bytes=64)
             if part < LOW_UNITS:
                 nc.vector.tensor_tensor(
-                    out=grouped[:].rearrange("p g n u e -> p (g n) u e"),
+                    out=grouped.rearrange("p g n u e -> p (g n) u e"),
                     in0=bank[:].bitcast(BF16).rearrange("p u g (n e) -> p (g n) u e", e=2),
                     in1=row_sign[:, blk]
                     .rearrange("p g n e -> p (g n) e")
@@ -292,29 +316,28 @@ def tile_bcnnresnet_k_kernel(tc, feat, W, b, out):
             else:
                 i0 = part * UNIT_ROWS - LOW
                 nc.vector.tensor_tensor(
-                    out=grouped[:],
+                    out=grouped,
                     in0=bank[:].bitcast(BF16).rearrange("p u g (n e) -> p g n u e", e=2),
                     in1=col_sign_of[blk][:, :, i0 : i0 + UNIT_ROWS].rearrange(
                         "p n (g u e) -> p g n u e", g=UNIT_PASSES, u=2
                     ),
                     op=ALU.mult,
                 )
-            return grouped
 
-        def quantise_x(grouped):
-            codes = codes_pool.tile([P, UNIT_PASSES, P], U32, name="x_codes", align_bytes=64)
-            scales = codes_pool.tile([P, UNIT_PASSES, P], U8, name="x_scales", align_bytes=64)
+        def quantise_x(grouped, count):
+            codes = codes_pool.tile([P, count * UNIT_PASSES, P], U32, name="x_codes", align_bytes=64)
+            scales = codes_pool.tile([P, count * UNIT_PASSES, P], U8, name="x_scales", align_bytes=64)
             nc.vector.quantize_mx(
                 out=codes[:].rearrange("p g n -> p (g n)").bitcast(FP8X4),
                 scales=scales[:].rearrange("p g n -> p (g n)"),
-                in_=grouped[:].rearrange("p g n u e -> p (g n u e)"),
+                in_=grouped[:].rearrange("p k g n u e -> p (k g n u e)"),
             )
             return codes, scales
 
         acc_of = {}
         passes_done = [0] * BLOCKS
 
-        def multiply(h, codes, scales):
+        def multiply(h, codes, scales, first):
             blk, part = divmod(h, UNITS_PER_BLOCK)
             if passes_done[blk] == 0:
                 acc_of[blk] = acc_pool.tile([P, C], F32, name="acc")
@@ -322,8 +345,8 @@ def tile_bcnnresnet_k_kernel(tc, feat, W, b, out):
                 k_pass = part * UNIT_PASSES + g
                 nc.tensor.matmul_mx(
                     out=acc_of[blk][:],
-                    lhsT=codes[:, g, :].bitcast(FP8X4),
-                    lhsT_scale=scales[:, g, :],
+                    lhsT=codes[:, first + g, :].bitcast(FP8X4),
+                    lhsT_scale=scales[:, first + g, :],
                     rhs=w_codes[:, k_pass, :].bitcast(FP8X4),
                     rhs_scale=w_scales[:, k_pass, :],
                     start=(passes_done[blk] == 0),
@@ -336,52 +359,58 @@ def tile_bcnnresnet_k_kernel(tc, feat, W, b, out):
             nc.vector.tensor_tensor(out=result[:], in0=acc_of[blk][:], in1=bias_rows[:], op=ALU.add)
             nc.sync.dma_start(out=out[blk * P : (blk + 1) * P, :], in_=result[:])
 
-        order = []
-        for blk in range(BLOCKS + 1):
-            low = [blk * UNITS_PER_BLOCK + k for k in range(LOW_UNITS)] if blk < BLOCKS else []
-            high = [(blk - 1) * UNITS_PER_BLOCK + LOW_UNITS + k for k in range(HIGH_UNITS)] if blk > 0 else []
-            if blk == BLOCKS:
-                order += high
+        made = [[h] for h in range(UNITS_PER_BLOCK)]
+        made += [[h, h + 1] for h in range(UNITS_PER_BLOCK, STEPS, 2)]
+        turned = {k + 1: [k] for k in range(LOW_UNITS)}
+        rounds = UNITS_PER_BLOCK
+        for blk in range(1, BLOCKS + 1):
+            low = [[blk * UNITS_PER_BLOCK + k, blk * UNITS_PER_BLOCK + k + 1] for k in range(0, LOW_UNITS, 2)]
+            high = [[blk * UNITS_PER_BLOCK - k, blk * UNITS_PER_BLOCK - k + 1] for k in range(HIGH_UNITS, 0, -2)]
+            if blk < BLOCKS:
+                line = []
+                while low or high:
+                    if high and len(line) % GAP == 0 or not low:
+                        line.append(high.pop(0))
+                    else:
+                        line.append(low.pop(0))
             else:
-                for k in range(LOW_UNITS):
-                    if k % 3 == 0 and high:
-                        order.append(high.pop(0))
-                    order.append(low[k])
-        unit_at = {}
-        step = 0
-        for h in order:
-            blk, part = divmod(h, UNITS_PER_BLOCK)
-            step = max(step + 1, blk * UNITS_PER_BLOCK + 1 + part if part < LOW_UNITS else (blk + 1) * UNITS_PER_BLOCK)
-            unit_at[step] = h
-        last_step = step
-        w_at = W_AT
-        bank_of, grouped_of, codes_of = {}, {}, {}
-        ready_w = 0
+                line = high
+            for pair in line:
+                turned[rounds] = pair
+                rounds += 1
+        last = rounds - 1
+        w_at = {s: w for w, s in enumerate(W_ROUNDS)}
+        high_at = {}
+        for k_pass, s in zip(range(2 * LOW_UNITS, PASSES), HIGH_TURN):
+            high_at.setdefault(s, []).append(k_pass)
+        bank_of, codes_of, grouped_of = {}, {}, {}
+        ready = 0
         waiting = []
         finish_at, finished = {}, []
-        transposed, copied, quantised = [], [], []
-        for step in range(last_step + 7):
-            w = w_at.get(step)
-            if w is not None:
-                if w not in w_bank_of:
-                    w_bank_of[w] = transpose_w(w)
-                w_grouped_of[w] = regroup_w(w, w_bank_of[w])
-            if step < STEPS:
-                take_roots(step)
-            if 1 <= step <= STEPS:
-                sign_rows(step - 1, True)
-            if step == 8:
+        for now in range(last + 6):
+            w = w_at.get(now)
+            if w is not None and w < WV:
+                w_grouped_of[w] = copy_w_rows(w, w_bank_of[w])
+            if now < len(made):
+                take_roots(made[now])
+            for k_pass in high_at.get(now - 1, []):
+                w_grouped_of[k_pass] = copy_w_high(w_bank_of[k_pass])
+            units = made[now - 1] if 1 <= now <= len(made) else []
+            blk = units[0] // UNITS_PER_BLOCK if units else 0
+            if units and units[0] % UNITS_PER_BLOCK < LOW_UNITS:
+                sign_rows(units, SC_ROWS[blk], GP_ROWS if len(units) > 1 else 0)
+            elif units:
+                sign_short_rows(units)
+            if now == 0:
+                spread_row_sign(0)
+            if now == 7:
+                park_signs()
+            if now == 8:
                 for blk in range(2):
                     load_col_sign(blk)
-            if step in (2 * UNITS_PER_BLOCK + 2, 3 * UNITS_PER_BLOCK + 2):
-                load_col_sign(step // UNITS_PER_BLOCK)
-            if 1 <= step <= STEPS:
-                sign_rows(step - 1, False)
-            if step == 0:
-                spread_row_sign(0)
-            if step == 7:
-                park_signs()
-            if step == 1:
+            if now in (25, 33):
+                load_col_sign((now - 9) // 8)
+            if now == 1:
                 nc.gpsimd.tensor_scalar(
                     out=sign_twice[:, 1:],
                     in0=sign_f32[:, 1:].unsqueeze(2).to_broadcast([P, BLOCKS - 1, 2, D]),
@@ -390,39 +419,47 @@ def tile_bcnnresnet_k_kernel(tc, feat, W, b, out):
                     op0=ALU.mult,
                     op1=ALU.add,
                 )
-            if step in (4, 5, 6):
-                scale_block(step - 3)
-                spread_row_sign(step - 3)
-            h = unit_at.get(step)
-            if h is not None:
+            if now in (4, 5, 6):
+                scale_block(now - 3)
+                spread_row_sign(now - 3)
+            for h in turned.get(now, []):
                 bank_of[h] = transpose_x(h)
-                transposed.append((step, h))
-            if step + 1 in w_at and w_at[step + 1] not in w_bank_of:
-                w_bank_of[w_at[step + 1]] = transpose_w(w_at[step + 1])
-            for blk in finish_at.get(step, []):
+            if w_at.get(now + 1, 0) > 0:
+                w_bank_of[w_at[now + 1]] = turn_w_rows(w_at[now + 1])
+            for k_pass in high_at.get(now, []):
+                w_bank_of[k_pass] = turn_w_high(k_pass)
+            for blk in finish_at.get(now, []):
                 finish_block(blk)
-            if transposed and transposed[0][0] <= step - LAG(transposed[0][0]):
-                h = transposed.pop(0)[1]
-                grouped_of[h] = regroup_x(h, bank_of[h])
-                copied.append((step, h))
-            if copied and copied[0][0] < step:
-                h = copied.pop(0)[1]
-                codes_of[h] = quantise_x(grouped_of[h])
-                waiting.append(h)
-            w = w_at.get(step - 1)
+            units = turned.get(now - 1, [])
+            if units:
+                grouped = grouped_pool.tile(
+                    [P, len(units), UNIT_PASSES, P, 2, 2], BF16, name="grouped", align_bytes=64
+                )
+                for k, h in enumerate(units):
+                    regroup_x(h, bank_of[h], grouped[:, k])
+                grouped_of[units[0]] = grouped
+            w = w_at.get(now)
+            if w is not None and w >= WV:
+                w_grouped_of[w] = copy_w_rows(w, w_bank_of[w])
+            units = turned.get(now - 2, [])
+            if units:
+                codes, scales = quantise_x(grouped_of[units[0]], len(units))
+                for k, h in enumerate(units):
+                    codes_of[h] = (codes, scales, k * UNIT_PASSES)
+                    waiting.append(h)
+            w = w_at.get(now - 1)
             if w is not None:
-                quantise_w(w, w_grouped_of[w])
-                ready_w = w + 1
-            now = [h for h in waiting if h % UNITS_PER_BLOCK < ready_w]
-            if len(now) >= MM_UNITS or step > last_step + 1:
-                for h in now:
-                    multiply(h, codes_of[h][0], codes_of[h][1])
+                quantise_w(2 * w, UNIT_PASSES, w_grouped_of[w])
+                ready = 2 * w + 2
+            for k_pass in high_at.get(now - 2, []):
+                quantise_w(k_pass, 1, w_grouped_of[k_pass])
+                ready = k_pass + 1
+            able = [h for h in waiting if UNIT_PASSES * (h % UNITS_PER_BLOCK + 1) <= ready]
+            if len(able) >= MM_UNITS or now >= last:
+                for h in able:
+                    multiply(h, *codes_of[h])
                     waiting.remove(h)
                 for blk in range(BLOCKS):
                     if passes_done[blk] == PASSES and blk not in finished:
-                        finish_at.setdefault(step + 2 if step < last_step else step + 1, []).append(blk)
+                        finish_at.setdefault(now + 1, []).append(blk)
                         finished.append(blk)
-        for later in sorted(finish_at):
-            if later >= last_step + 7:
-                for blk in finish_at[later]:
-                    finish_block(blk)

@@ -29,17 +29,17 @@ LOW_UNITS = LOW // UNIT_ROWS
 HIGH_UNITS = HIGH // UNIT_ROWS
 STEPS = BLOCKS * UNITS_PER_BLOCK
 W_LOADS = 8
-GAP = 3
-HPER = 2
-HA = 28
+GAP = 4
+HPER = 1
+HA = 18
 HN = 8
-HB = 34
+HB = 32
 WA = 12
 WB = 12
 WS = 1
 WV = 99
 GP_ROWS = 0
-SC_ROWS = (0, 0, 0, 0)
+SC_ROWS = (0, 0, 0, 4)
 MM_UNITS = 4
 X_BANKS = 4
 W_BANKS = 1
@@ -124,15 +124,15 @@ def tile_bcnnresnet_k_kernel(tc, feat, W, b, out):
         def turn_w_high(k_pass):
             passes_per_load = PASSES // W_LOADS
             rows = w_rows[k_pass // passes_per_load]
-            bank = w_bank_pool.tile([P, P, 4], F32, name="bank")
+            bank = w_bank_pool.tile([P, 4, P], BF16, name="bank")
             for t in range(4):
                 at = (k_pass % passes_per_load) * K_PASS + t * D
-                nc.tensor.matmul(out=bank[:, :, t], lhsT=rows[:, at : at + D], rhs=ident_bf[:], start=True, stop=True)
+                nc.tensor.transpose(out=bank[:, t, :], in_=rows[:, at : at + D], identity=ident_bf[:])
             return bank
 
         def copy_w_high(bank):
             grouped = grouped_pool.tile([P, 1, C, 4], BF16, name="w_grouped", align_bytes=64)
-            nc.scalar.copy(out=grouped[:, 0], in_=bank[:])
+            nc.scalar.copy(out=grouped[:, 0], in_=bank[:].rearrange("p t c -> p c t"))
             return grouped
 
         def quantise_w(k_pass, passes, grouped):

@@ -29,20 +29,25 @@ LOW_UNITS = LOW // UNIT_ROWS
 HIGH_UNITS = HIGH // UNIT_ROWS
 STEPS = BLOCKS * UNITS_PER_BLOCK
 W_LOADS = 8
-GAP = 4
+GAP = 2
+WL = 2
+HL = 1
+AQ = 99
+QS = 0
+WFIRST = True
 HPER = 1
-HA = 18
+HA = 22
 HN = 8
-HB = 32
+HB = 36
 WA = 12
 WB = 12
 WS = 1
 WV = 99
-GP_ROWS = 0
-SC_ROWS = (0, 0, 0, 4)
+GP_ROWS = 3
+SC_ROWS = (0, 0, 0, 3)
 MM_UNITS = 4
-X_BANKS = 4
-W_BANKS = 1
+X_BANKS = 3
+W_BANKS = 2
 ACCS = 3
 HIGH_TURN = [HA + j // HPER if j < HN else HB + (j - HN) // HPER for j in range(4 * HIGH_UNITS // 2)]
 W_ROUNDS = [w if w < WA else WB + WS * (w - WA) for w in range(LOW_UNITS)]
@@ -60,7 +65,7 @@ def tile_bcnnresnet_k_kernel(tc, feat, W, b, out):
         table_pool = ctx.enter_context(tc.tile_pool(name="table_pool", bufs=2))
         col_sign_pool = ctx.enter_context(tc.tile_pool(name="col_sign_pool", bufs=2))
         grouped_pool = ctx.enter_context(tc.tile_pool(name="grouped_pool", bufs=3))
-        codes_pool = ctx.enter_context(tc.tile_pool(name="codes_pool", bufs=10))
+        codes_pool = ctx.enter_context(tc.tile_pool(name="codes_pool", bufs=16))
         out_pool = ctx.enter_context(tc.tile_pool(name="out_pool", bufs=2))
         banks_pool = ctx.enter_context(tc.psum_pool(name="banks_pool", bufs=X_BANKS))
         w_bank_pool = ctx.enter_context(tc.psum_pool(name="w_bank_pool", bufs=W_BANKS))
@@ -361,7 +366,7 @@ def tile_bcnnresnet_k_kernel(tc, feat, W, b, out):
 
         made = [[h] for h in range(UNITS_PER_BLOCK)]
         made += [[h, h + 1] for h in range(UNITS_PER_BLOCK, STEPS, 2)]
-        turned = {k + 1: [k] for k in range(LOW_UNITS)}
+        turned = {k + 1 + k // AQ: [k] for k in range(LOW_UNITS)}
         rounds = UNITS_PER_BLOCK
         for blk in range(1, BLOCKS + 1):
             low = [[blk * UNITS_PER_BLOCK + k, blk * UNITS_PER_BLOCK + k + 1] for k in range(0, LOW_UNITS, 2)]
@@ -387,13 +392,20 @@ def tile_bcnnresnet_k_kernel(tc, feat, W, b, out):
         ready = 0
         waiting = []
         finish_at, finished = {}, []
+        def turn_w(now):
+            for s, w in w_at.items():
+                if w > 0 and now == max(0, s - WL):
+                    w_bank_of[w] = turn_w_rows(w)
+            for k_pass in high_at.get(now, []):
+                w_bank_of[k_pass] = turn_w_high(k_pass)
+
         for now in range(last + 6):
             w = w_at.get(now)
             if w is not None and w < WV:
                 w_grouped_of[w] = copy_w_rows(w, w_bank_of[w])
             if now < len(made):
                 take_roots(made[now])
-            for k_pass in high_at.get(now - 1, []):
+            for k_pass in high_at.get(now - HL, []):
                 w_grouped_of[k_pass] = copy_w_high(w_bank_of[k_pass])
             units = made[now - 1] if 1 <= now <= len(made) else []
             blk = units[0] // UNITS_PER_BLOCK if units else 0
@@ -422,12 +434,12 @@ def tile_bcnnresnet_k_kernel(tc, feat, W, b, out):
             if now in (4, 5, 6):
                 scale_block(now - 3)
                 spread_row_sign(now - 3)
+            if WFIRST:
+                turn_w(now)
             for h in turned.get(now, []):
                 bank_of[h] = transpose_x(h)
-            if w_at.get(now + 1, 0) > 0:
-                w_bank_of[w_at[now + 1]] = turn_w_rows(w_at[now + 1])
-            for k_pass in high_at.get(now, []):
-                w_bank_of[k_pass] = turn_w_high(k_pass)
+            if not WFIRST:
+                turn_w(now)
             for blk in finish_at.get(now, []):
                 finish_block(blk)
             units = turned.get(now - 1, [])
@@ -451,7 +463,7 @@ def tile_bcnnresnet_k_kernel(tc, feat, W, b, out):
             if w is not None:
                 quantise_w(2 * w, UNIT_PASSES, w_grouped_of[w])
                 ready = 2 * w + 2
-            for k_pass in high_at.get(now - 2, []):
+            for k_pass in high_at.get(now - HL - 1, []):
                 quantise_w(k_pass, 1, w_grouped_of[k_pass])
                 ready = k_pass + 1
             able = [h for h in waiting if UNIT_PASSES * (h % UNITS_PER_BLOCK + 1) <= ready]

@@ -29,22 +29,26 @@ LOW_UNITS = LOW // UNIT_ROWS
 HIGH_UNITS = HIGH // UNIT_ROWS
 STEPS = BLOCKS * UNITS_PER_BLOCK
 W_LOADS = 8
-GAP = 2
+GAP = 3
 WL = 2
 HL = 1
 AQ = 99
+G0 = 0
+FINLAG = 2
+SPREAD = [8, 9, 10]
+LATE0 = False
 QS = 0
-WFIRST = True
+WFIRST = False
 HPER = 1
-HA = 22
+HA = 20
 HN = 8
-HB = 36
+HB = 26
 WA = 12
 WB = 12
 WS = 1
-WV = 99
-GP_ROWS = 3
-SC_ROWS = (0, 0, 0, 3)
+WVSET = (0, 1)
+GP_ROWS = 4
+SC_ROWS = (0, 0, 0, 2)
 MM_UNITS = 4
 X_BANKS = 3
 W_BANKS = 2
@@ -120,7 +124,7 @@ def tile_bcnnresnet_k_kernel(tc, feat, W, b, out):
             grouped = grouped_pool.tile([P, UNIT_PASSES, C, 4], BF16, name="w_grouped", align_bytes=64)
             words_out = grouped[:].rearrange("p g c t -> p (g c) t").bitcast(F32)
             words_in = bank[:].rearrange("p u g c -> p (g c) u")
-            if w < WV:
+            if w not in WVSET:
                 nc.scalar.copy(out=words_out, in_=words_in)
             else:
                 nc.vector.tensor_copy(out=words_out, in_=words_in)
@@ -401,16 +405,18 @@ def tile_bcnnresnet_k_kernel(tc, feat, W, b, out):
 
         for now in range(last + 6):
             w = w_at.get(now)
-            if w is not None and w < WV:
+            if w is not None and w not in WVSET and not (LATE0 and now == 0):
                 w_grouped_of[w] = copy_w_rows(w, w_bank_of[w])
             if now < len(made):
                 take_roots(made[now])
+            if LATE0 and now == 0 and 0 not in WVSET:
+                w_grouped_of[0] = copy_w_rows(0, w_bank_of[0])
             for k_pass in high_at.get(now - HL, []):
                 w_grouped_of[k_pass] = copy_w_high(w_bank_of[k_pass])
             units = made[now - 1] if 1 <= now <= len(made) else []
             blk = units[0] // UNITS_PER_BLOCK if units else 0
             if units and units[0] % UNITS_PER_BLOCK < LOW_UNITS:
-                sign_rows(units, SC_ROWS[blk], GP_ROWS if len(units) > 1 else 0)
+                sign_rows(units, SC_ROWS[blk], GP_ROWS if len(units) > 1 else G0)
             elif units:
                 sign_short_rows(units)
             if now == 0:
@@ -433,7 +439,8 @@ def tile_bcnnresnet_k_kernel(tc, feat, W, b, out):
                 )
             if now in (4, 5, 6):
                 scale_block(now - 3)
-                spread_row_sign(now - 3)
+            if now in SPREAD:
+                spread_row_sign(SPREAD.index(now) + 1)
             if WFIRST:
                 turn_w(now)
             for h in turned.get(now, []):
@@ -451,7 +458,7 @@ def tile_bcnnresnet_k_kernel(tc, feat, W, b, out):
                     regroup_x(h, bank_of[h], grouped[:, k])
                 grouped_of[units[0]] = grouped
             w = w_at.get(now)
-            if w is not None and w >= WV:
+            if w is not None and w in WVSET:
                 w_grouped_of[w] = copy_w_rows(w, w_bank_of[w])
             units = turned.get(now - 2, [])
             if units:
@@ -473,5 +480,5 @@ def tile_bcnnresnet_k_kernel(tc, feat, W, b, out):
                     waiting.remove(h)
                 for blk in range(BLOCKS):
                     if passes_done[blk] == PASSES and blk not in finished:
-                        finish_at.setdefault(now + 1, []).append(blk)
+                        finish_at.setdefault(now + (FINLAG if now < last else 1), []).append(blk)
                         finished.append(blk)

from contextlib import ExitStack

import concourse.mybir as mybir
from concourse.masks import make_identity

F32 = mybir.dt.float32
BF16 = mybir.dt.bfloat16
U32 = mybir.dt.uint32
U8 = mybir.dt.uint8
FP8X4 = mybir.dt.float8_e4m3fn_x4
ALU = mybir.AluOpType
FUNC = mybir.ActivationFunctionType
AXIS = mybir.AxisListType

P = 128
B, D, C = 512, 128, 128
LOW = 96
HIGH = D - LOW
EPS_SQRT = 1e-10
EPS_NORM = 1e-12

BLOCKS = B // P
K_PASS = 4 * P
PASSES = D * D // K_PASS
UNIT_PASSES = 2
UNIT_ROWS = 8
UNITS_PER_BLOCK = PASSES // UNIT_PASSES
LOW_UNITS = LOW // UNIT_ROWS
HIGH_UNITS = HIGH // UNIT_ROWS
STEPS = BLOCKS * UNITS_PER_BLOCK
W_LOADS = 8
GAP = 3
WL = 2
HL = 1
AQ = 99
G0 = 0
FINLAG = 2
SPREAD = [8, 9, 10]
LATE0 = False
QS = 0
WFIRST = False
HPER = 1
HA = 20
HN = 8
HB = 26
WA = 12
WB = 12
WS = 1
WVSET = (0, 1)
GP_ROWS = 4
SC_ROWS = (0, 0, 0, 2)
MM_UNITS = 4
X_BANKS = 3
W_BANKS = 2
ACCS = 3
HIGH_TURN = [HA + j // HPER if j < HN else HB + (j - HN) // HPER for j in range(4 * HIGH_UNITS // 2)]
W_ROUNDS = [w if w < WA else WB + WS * (w - WA) for w in range(LOW_UNITS)]

FLOPS = 2 * B * D * D * C


def tile_bcnnresnet_k_kernel(tc, feat, W, b, out):
    nc = tc.nc
    with ExitStack() as ctx:
        ctx.enter_context(tc.manual_schedule())
        keep = ctx.enter_context(tc.tile_pool(name="keep", bufs=1))
        w_in = ctx.enter_context(tc.tile_pool(name="w_in", bufs=W_LOADS))
        raw_pool = ctx.enter_context(tc.tile_pool(name="raw_pool", bufs=4))
        table_pool = ctx.enter_context(tc.tile_pool(name="table_pool", bufs=2))
        col_sign_pool = ctx.enter_context(tc.tile_pool(name="col_sign_pool", bufs=2))
        grouped_pool = ctx.enter_context(tc.tile_pool(name="grouped_pool", bufs=3))
        codes_pool = ctx.enter_context(tc.tile_pool(name="codes_pool", bufs=16))
        out_pool = ctx.enter_context(tc.tile_pool(name="out_pool", bufs=2))
        banks_pool = ctx.enter_context(tc.psum_pool(name="banks_pool", bufs=X_BANKS))
        w_bank_pool = ctx.enter_context(tc.psum_pool(name="w_bank_pool", bufs=W_BANKS))
        acc_pool = ctx.enter_context(tc.psum_pool(name="acc_pool", bufs=ACCS))

        feat_sb = keep.tile([P, BLOCKS, D], BF16, name="feat_sb")
        nc.sync.dma_start(out=feat_sb[:], in_=feat.rearrange("(blk p) d -> p blk d", p=P))
        load_cols = D * D // W_LOADS
        w_rows = []
        for q in range(W_LOADS):
            rows = w_in.tile([P, load_cols], BF16, name="w_rows")
            nc.sync.dma_start(out=rows[:], in_=W[:, q * load_cols : (q + 1) * load_cols])
            w_rows.append(rows)
        bias_rows = keep.tile([P, C], BF16, name="bias_rows")
        nc.sync.dma_start(out=bias_rows[:], in_=b.partition_broadcast(P))

        ident = keep.tile([P, P], F32, name="ident")
        make_identity(nc, ident[:])
        ident_bf = keep.tile([P, P], BF16, name="ident_bf")
        make_identity(nc, ident_bf[:])

        one = keep.tile([P, 1], F32, name="one")
        nc.vector.memset(one[:], 1.0)
        warm = keep.tile([P, 1], F32, name="warm")
        nc.scalar.activation(out=warm[:], in_=one[:], func=FUNC.Sqrt)

        w_codes = keep.tile([P, PASSES, C], U32, name="w_codes", align_bytes=64)
        w_scales = keep.tile([P, PASSES, C], U8, name="w_scales", align_bytes=64)

        def transpose_rows(words, pool):
            bank = pool.tile([P, 2, UNIT_PASSES, P], F32, name="bank")
            for g in range(UNIT_PASSES):
                for u in range(2):
                    first = (2 * g + u) * P
                    nc.tensor.transpose(out=bank[:, u, g, :], in_=words[:, first : first + P], identity=ident[:])
            return bank

        def transpose_cols(table, i0):
            words = table[:].rearrange("p m c -> p (m c)").bitcast(F32).rearrange("p (m w) -> p m w", m=D)
            bank = banks_pool.tile([P, 2, UNIT_PASSES, P], F32, name="bank")
            for g in range(UNIT_PASSES):
                for u in range(2):
                    nc.tensor.transpose(out=bank[:, u, g, :], in_=words[:, :, i0 // 2 + 2 * g + u], identity=ident[:])
            return bank

        def turn_w_rows(w):
            per_load = UNITS_PER_BLOCK // W_LOADS
            first = (w % per_load) * UNIT_ROWS * D
            return transpose_rows(w_rows[w // per_load][:, first : first + UNIT_ROWS * D].bitcast(F32), w_bank_pool)

        def copy_w_rows(w, bank):
            grouped = grouped_pool.tile([P, UNIT_PASSES, C, 4], BF16, name="w_grouped", align_bytes=64)
            words_out = grouped[:].rearrange("p g c t -> p (g c) t").bitcast(F32)
            words_in = bank[:].rearrange("p u g c -> p (g c) u")
            if w not in WVSET:
                nc.scalar.copy(out=words_out, in_=words_in)
            else:
                nc.vector.tensor_copy(out=words_out, in_=words_in)
            return grouped

        def turn_w_high(k_pass):
            passes_per_load = PASSES // W_LOADS
            rows = w_rows[k_pass // passes_per_load]
            bank = w_bank_pool.tile([P, 4, P], BF16, name="bank")
            for t in range(4):
                at = (k_pass % passes_per_load) * K_PASS + t * D
                nc.tensor.transpose(out=bank[:, t, :], in_=rows[:, at : at + D], identity=ident_bf[:])
            return bank

        def copy_w_high(bank):
            grouped = grouped_pool.tile([P, 1, C, 4], BF16, name="w_grouped", align_bytes=64)
            nc.scalar.copy(out=grouped[:, 0], in_=bank[:].rearrange("p t c -> p c t"))
            return grouped

        def quantise_w(k_pass, passes, grouped):
            span = slice(k_pass, k_pass + passes)
            nc.vector.quantize_mx(
                out=w_codes[:, span, :].rearrange("p g c -> p (g c)").bitcast(FP8X4),
                scales=w_scales[:, span, :].rearrange("p g c -> p (g c)"),
                in_=grouped[:].rearrange("p g c t -> p (g c t)"),
            )

        mag = keep.tile([P, BLOCKS, D], BF16, name="mag")
        sum_mag = keep.tile([P, BLOCKS], F32, name="sum_mag")
        for blk in range(BLOCKS):
            nc.scalar.activation(
                out=mag[:, blk, :], in_=feat_sb[:, blk, :], func=FUNC.Abs, accum_out=sum_mag[:, blk : blk + 1]
            )

        nonzero = keep.tile([P, BLOCKS, D], BF16, name="nonzero")
        nc.vector.tensor_single_scalar(out=nonzero[:], in_=feat_sb[:], scalar=0.0, op=ALU.not_equal)
        negative = keep.tile([P, BLOCKS, D], BF16, name="negative")
        nc.vector.tensor_single_scalar(out=negative[:], in_=feat_sb[:], scalar=0.0, op=ALU.is_lt)
        count = keep.tile([P, BLOCKS], F32, name="count")
        nc.vector.tensor_reduce(out=count[:], in_=nonzero[:], axis=AXIS.X, op=ALU.add)
        sign_f32 = keep.tile([P, BLOCKS, D], F32, name="sign_f32")
        nc.vector.scalar_tensor_tensor(
            out=sign_f32[:, 0], in0=feat_sb[:, 0], scalar=0.0, in1=negative[:, 0], op0=ALU.is_gt, op1=ALU.subtract
        )
        eps_count = keep.tile([P, BLOCKS], F32, name="eps_count")
        nc.vector.scalar_tensor_tensor(
            out=eps_count[:], in0=count[:], scalar=EPS_SQRT, in1=count[:], op0=ALU.mult, op1=ALU.mult
        )
        sum_sq = keep.tile([P, BLOCKS], F32, name="sum_sq")
        nc.vector.tensor_tensor(out=sum_sq[:], in0=sum_mag[:], in1=sum_mag[:], op=ALU.mult)
        norm_sq = keep.tile([P, BLOCKS], F32, name="norm_sq")
        nc.vector.scalar_tensor_tensor(
            out=norm_sq[:], in0=eps_count[:], scalar=EPS_NORM * EPS_NORM, in1=sum_sq[:], op0=ALU.max, op1=ALU.add
        )
        inv_norm_sq = keep.tile([P, BLOCKS], F32, name="inv_norm_sq")
        nc.vector.reciprocal(out=inv_norm_sq[:], in_=norm_sq[:])
        row_scale = keep.tile([P, BLOCKS, D], F32, name="row_scale")

        def scale_block(blk):
            nc.vector.tensor_scalar_mul(
                out=row_scale[:, blk, :], in0=mag[:, blk, :], scalar1=inv_norm_sq[:, blk : blk + 1]
            )

        scale_block(0)
        eps_scaled = keep.tile([P, BLOCKS], F32, name="eps_scaled")
        nc.vector.tensor_scalar_mul(out=eps_scaled[:], in0=inv_norm_sq[:], scalar1=EPS_SQRT)

        sign_twice = keep.tile([P, BLOCKS, 2, D], BF16, name="sign_twice")
        nc.vector.tensor_copy(out=sign_twice[:, 0], in_=sign_f32[:, 0].unsqueeze(1).to_broadcast([P, 2, D]))
        nc.vector.scalar_tensor_tensor(
            out=sign_f32[:, 1:], in0=feat_sb[:, 1:], scalar=0.0, in1=negative[:, 1:], op0=ALU.is_gt, op1=ALU.subtract
        )

        w_bank_of, w_grouped_of = {}, {}
        w_bank_of[0] = turn_w_rows(0)
        row_sign = keep.tile([P, BLOCKS, UNIT_PASSES, P, 2], BF16, name="row_sign")

        def spread_row_sign(blk):
            bank = banks_pool.tile([P, P], F32, name="bank")
            nc.tensor.transpose(
                out=bank[:], in_=sign_twice[:, blk].rearrange("p h d -> p (h d)").bitcast(F32), identity=ident[:]
            )
            nc.vector.tensor_copy(
                out=row_sign[:, blk].rearrange("p g n e -> p g (n e)").bitcast(F32),
                in_=bank[:].unsqueeze(1).to_broadcast([P, UNIT_PASSES, P]),
            )

        sign_high = keep.tile([P, BLOCKS, HIGH], BF16, name="sign_high")
        words_high = P * HIGH // 2
        parked = out[(BLOCKS - 1) * P : (BLOCKS - 1) * P + BLOCKS * words_high // C, :].rearrange("r c -> (r c)")

        sign_pairs = keep.tile([P, BLOCKS, HIGH, 2], BF16, name="sign_pairs")

        def park_signs():
            nc.vector.tensor_copy(out=sign_high[:], in_=sign_f32[:, :, LOW:])
            nc.gpsimd.tensor_scalar(
                out=sign_pairs[:],
                in0=sign_f32[:, :, LOW:].unsqueeze(3).to_broadcast([P, BLOCKS, HIGH, 2]),
                scalar1=1.0,
                scalar2=0.0,
                op0=ALU.mult,
                op1=ALU.add,
            )
            nc.sync.dma_start(
                out=parked.rearrange("(blk n w) -> n blk w", blk=BLOCKS, n=P), in_=sign_high[:].bitcast(F32)
            )

        col_sign_of = {}

        def load_col_sign(blk):
            col_sign = col_sign_pool.tile([P, P, HIGH], BF16, name="col_sign")
            nc.sync.dma_start(
                out=col_sign[:].rearrange("p n i -> p (n i)").bitcast(F32),
                in_=parked[blk * words_high : (blk + 1) * words_high].partition_broadcast(P),
            )
            col_sign_of[blk] = col_sign

        table_of, raw_of = {}, {}

        def take_roots(units):
            blk, part = divmod(units[0], UNITS_PER_BLOCK)
            if part == 0:
                table_of[blk] = table_pool.tile([P, D, D], BF16, name="table")
            rows = range(part * UNIT_ROWS, (part + len(units)) * UNIT_ROWS)
            if rows[0] < LOW:
                raw_of[units[0]] = raw_pool.tile([P, 2 * UNIT_ROWS, D], BF16, name="raw")
            for i in rows:
                nc.scalar.activation(
                    out=raw_of[units[0]][:, i - rows[0], :] if i < LOW else table_of[blk][:, i, LOW:],
                    in_=mag[:, blk, :] if i < LOW else mag[:, blk, LOW:],
                    func=FUNC.Sqrt,
                    scale=row_scale[:, blk, i : i + 1],
                    bias=eps_scaled[:, blk : blk + 1],
                )

        def sign_short_rows(units):
            blk, part = divmod(units[0], UNITS_PER_BLOCK)
            rows = slice(part * UNIT_ROWS, (part + len(units)) * UNIT_ROWS)
            count = len(units) * UNIT_ROWS
            short = table_of[blk][:, rows, LOW:].rearrange("p s (w e) -> p s w e", e=2)
            factors = sign_pairs[:, blk, rows.start - LOW : rows.stop - LOW, :]
            nc.vector.tensor_tensor(
                out=short,
                in0=short,
                in1=factors.unsqueeze(2).to_broadcast([P, count, HIGH // 2, 2]),
                op=ALU.mult,
            )

        def sign_rows(units, by_scalar, by_gpsimd):
            blk, part = divmod(units[0], UNITS_PER_BLOCK)
            first = part * UNIT_ROWS
            count = len(units) * UNIT_ROWS
            raw = raw_of[units[0]][:].rearrange("p s d -> p (s d)")
            table = table_of[blk][:, first : first + count, :].rearrange("p s d -> p (s d)")
            for s in range(by_scalar):
                nc.scalar.activation(
                    out=table[:, s * D : (s + 1) * D],
                    in_=raw[:, s * D : (s + 1) * D],
                    func=FUNC.Copy,
                    scale=sign_f32[:, blk, first + s : first + s + 1],
                )
            for s in range(by_scalar, count - by_gpsimd):
                span = slice(s * D, (s + 1) * D + (2 if by_gpsimd and s == count - by_gpsimd - 1 else 0))
                nc.vector.tensor_scalar_mul(
                    out=table[:, span], in0=raw[:, span], scalar1=sign_f32[:, blk, first + s : first + s + 1]
                )
            for s in range(count - by_gpsimd, count):
                nc.gpsimd.tensor_scalar(
                    out=table[:, s * D : (s + 1) * D],
                    in0=raw[:, s * D : (s + 1) * D],
                    scalar1=sign_f32[:, blk, first + s : first + s + 1],
                    scalar2=0.0,
                    op0=ALU.mult,
                    op1=ALU.add,
                )

        def transpose_x(h):
            blk, part = divmod(h, UNITS_PER_BLOCK)
            i0 = part * UNIT_ROWS
            if part < LOW_UNITS:
                return transpose_rows(
                    table_of[blk][:, i0 : i0 + UNIT_ROWS, :].rearrange("p s d -> p (s d)").bitcast(F32), banks_pool
                )
            return transpose_cols(table_of[blk], i0)

        def regroup_x(h, bank, grouped):
            blk, part = divmod(h, UNITS_PER_BLOCK)
            if part < LOW_UNITS:
                nc.vector.tensor_tensor(
                    out=grouped.rearrange("p g n u e -> p (g n) u e"),
                    in0=bank[:].bitcast(BF16).rearrange("p u g (n e) -> p (g n) u e", e=2),
                    in1=row_sign[:, blk]
                    .rearrange("p g n e -> p (g n) e")
                    .unsqueeze(2)
                    .to_broadcast([P, UNIT_PASSES * P, 2, 2]),
                    op=ALU.mult,
                )
            else:
                i0 = part * UNIT_ROWS - LOW
                nc.vector.tensor_tensor(
                    out=grouped,
                    in0=bank[:].bitcast(BF16).rearrange("p u g (n e) -> p g n u e", e=2),
                    in1=col_sign_of[blk][:, :, i0 : i0 + UNIT_ROWS].rearrange(
                        "p n (g u e) -> p g n u e", g=UNIT_PASSES, u=2
                    ),
                    op=ALU.mult,
                )

        def quantise_x(grouped, count):
            codes = codes_pool.tile([P, count * UNIT_PASSES, P], U32, name="x_codes", align_bytes=64)
            scales = codes_pool.tile([P, count * UNIT_PASSES, P], U8, name="x_scales", align_bytes=64)
            nc.vector.quantize_mx(
                out=codes[:].rearrange("p g n -> p (g n)").bitcast(FP8X4),
                scales=scales[:].rearrange("p g n -> p (g n)"),
                in_=grouped[:].rearrange("p k g n u e -> p (k g n u e)"),
            )
            return codes, scales

        acc_of = {}
        passes_done = [0] * BLOCKS

        def multiply(h, codes, scales, first):
            blk, part = divmod(h, UNITS_PER_BLOCK)
            if passes_done[blk] == 0:
                acc_of[blk] = acc_pool.tile([P, C], F32, name="acc")
            for g in range(UNIT_PASSES):
                k_pass = part * UNIT_PASSES + g
                nc.tensor.matmul_mx(
                    out=acc_of[blk][:],
                    lhsT=codes[:, first + g, :].bitcast(FP8X4),
                    lhsT_scale=scales[:, first + g, :],
                    rhs=w_codes[:, k_pass, :].bitcast(FP8X4),
                    rhs_scale=w_scales[:, k_pass, :],
                    start=(passes_done[blk] == 0),
                    stop=(passes_done[blk] == PASSES - 1),
                )
                passes_done[blk] += 1

        def finish_block(blk):
            result = out_pool.tile([P, C], F32, name="result")
            nc.vector.tensor_tensor(out=result[:], in0=acc_of[blk][:], in1=bias_rows[:], op=ALU.add)
            nc.sync.dma_start(out=out[blk * P : (blk + 1) * P, :], in_=result[:])

        made = [[h] for h in range(UNITS_PER_BLOCK)]
        made += [[h, h + 1] for h in range(UNITS_PER_BLOCK, STEPS, 2)]
        turned = {k + 1 + k // AQ: [k] for k in range(LOW_UNITS)}
        rounds = UNITS_PER_BLOCK
        for blk in range(1, BLOCKS + 1):
            low = [[blk * UNITS_PER_BLOCK + k, blk * UNITS_PER_BLOCK + k + 1] for k in range(0, LOW_UNITS, 2)]
            high = [[blk * UNITS_PER_BLOCK - k, blk * UNITS_PER_BLOCK - k + 1] for k in range(HIGH_UNITS, 0, -2)]
            if blk < BLOCKS:
                line = []
                while low or high:
                    if high and len(line) % GAP == 0 or not low:
                        line.append(high.pop(0))
                    else:
                        line.append(low.pop(0))
            else:
                line = high
            for pair in line:
                turned[rounds] = pair
                rounds += 1
        last = rounds - 1
        w_at = {s: w for w, s in enumerate(W_ROUNDS)}
        high_at = {}
        for k_pass, s in zip(range(2 * LOW_UNITS, PASSES), HIGH_TURN):
            high_at.setdefault(s, []).append(k_pass)
        bank_of, codes_of, grouped_of = {}, {}, {}
        ready = 0
        waiting = []
        finish_at, finished = {}, []
        def turn_w(now):
            for s, w in w_at.items():
                if w > 0 and now == max(0, s - WL):
                    w_bank_of[w] = turn_w_rows(w)
            for k_pass in high_at.get(now, []):
                w_bank_of[k_pass] = turn_w_high(k_pass)

        for now in range(last + 6):
            w = w_at.get(now)
            if w is not None and w not in WVSET and not (LATE0 and now == 0):
                w_grouped_of[w] = copy_w_rows(w, w_bank_of[w])
            if now < len(made):
                take_roots(made[now])
            if LATE0 and now == 0 and 0 not in WVSET:
                w_grouped_of[0] = copy_w_rows(0, w_bank_of[0])
            for k_pass in high_at.get(now - HL, []):
                w_grouped_of[k_pass] = copy_w_high(w_bank_of[k_pass])
            units = made[now - 1] if 1 <= now <= len(made) else []
            blk = units[0] // UNITS_PER_BLOCK if units else 0
            if units and units[0] % UNITS_PER_BLOCK < LOW_UNITS:
                sign_rows(units, SC_ROWS[blk], GP_ROWS if len(units) > 1 else G0)
            elif units:
                sign_short_rows(units)
            if now == 0:
                spread_row_sign(0)
            if now == 7:
                park_signs()
            if now == 8:
                for blk in range(2):
                    load_col_sign(blk)
            if now in (25, 33):
                load_col_sign((now - 9) // 8)
            if now == 1:
                nc.gpsimd.tensor_scalar(
                    out=sign_twice[:, 1:],
                    in0=sign_f32[:, 1:].unsqueeze(2).to_broadcast([P, BLOCKS - 1, 2, D]),
                    scalar1=1.0,
                    scalar2=0.0,
                    op0=ALU.mult,
                    op1=ALU.add,
                )
            if now in (4, 5, 6):
                scale_block(now - 3)
            if now in SPREAD:
                spread_row_sign(SPREAD.index(now) + 1)
            if WFIRST:
                turn_w(now)
            for h in turned.get(now, []):
                bank_of[h] = transpose_x(h)
            if not WFIRST:
                turn_w(now)
            for blk in finish_at.get(now, []):
                finish_block(blk)
            units = turned.get(now - 1, [])
            if units:
                grouped = grouped_pool.tile(
                    [P, len(units), UNIT_PASSES, P, 2, 2], BF16, name="grouped", align_bytes=64
                )
                for k, h in enumerate(units):
                    regroup_x(h, bank_of[h], grouped[:, k])
                grouped_of[units[0]] = grouped
            w = w_at.get(now)
            if w is not None and w in WVSET:
                w_grouped_of[w] = copy_w_rows(w, w_bank_of[w])
            units = turned.get(now - 2, [])
            if units:
                codes, scales = quantise_x(grouped_of[units[0]], len(units))
                for k, h in enumerate(units):
                    codes_of[h] = (codes, scales, k * UNIT_PASSES)
                    waiting.append(h)
            w = w_at.get(now - 1)
            if w is not None:
                quantise_w(2 * w, UNIT_PASSES, w_grouped_of[w])
                ready = 2 * w + 2
            for k_pass in high_at.get(now - HL - 1, []):
                quantise_w(k_pass, 1, w_grouped_of[k_pass])
                ready = k_pass + 1
            able = [h for h in waiting if UNIT_PASSES * (h % UNITS_PER_BLOCK + 1) <= ready]
            if len(able) >= MM_UNITS or now >= last:
                for h in able:
                    multiply(h, *codes_of[h])
                    waiting.remove(h)
                for blk in range(BLOCKS):
                    if passes_done[blk] == PASSES and blk not in finished:
                        finish_at.setdefault(now + (FINLAG if now < last else 1), []).append(blk)
                        finished.append(blk)
